import numpy as np
import ml_dtypes


def mxq(x, axis, fmt="e4m3"):
    dtype, down = {"e4m3": (ml_dtypes.float8_e4m3fn, 7), "e5m2": (ml_dtypes.float8_e5m2, 14)}[fmt]
    v = np.moveaxis(np.asarray(x, np.float32).astype(ml_dtypes.bfloat16).astype(np.float64), axis, -1)
    blocks = v.reshape(v.shape[:-1] + (-1, 32))
    amax = np.abs(blocks).max(-1, keepdims=True)
    byte = np.maximum(np.where(amax > 0, np.frexp(amax)[1] - 1 + 127, 0) - down, 1)
    scale = np.exp2(byte - 127.0)
    codes = (blocks / scale).astype(np.float32).astype(dtype).astype(np.float64)
    return np.moveaxis((codes * scale).reshape(v.shape), -1, axis)


WIDE = False


def mx_kscale(k):
    if not WIDE:
        return np.ones(k)
    levels = np.array([10, -10, 5, -5, 0])
    if k % 512:
        return np.exp2(np.random.permutation(np.resize(levels, k // 32))).repeat(32)
    a = np.empty((k // 512, 16))
    for p in range(k // 512):
        a[p, :8] = np.random.permutation(np.resize(levels, 8))
        for g in range(8):
            far = levels[np.abs(levels - a[p, g]) >= 10]
            a[p, g + 8] = far[np.random.randint(len(far))]
    return np.exp2(a.ravel()).repeat(32)


BF16 = ml_dtypes.bfloat16


def bf(x):
    return np.asarray(x, np.float32).astype(BF16)


def f64(x):
    return np.asarray(x).astype(np.float64)


B, N, H, D, C, O = 512, 24, 512, 512, 512, 512
F = D + D + C


def setup_inputs():
    s = mx_kscale(F)
    t = mx_kscale(H)
    ri, rt = mx_kscale(H), mx_kscale(H)
    return {
        "input_text": bf(np.random.standard_normal((B, D)) * s[:D])[:, None, :],
        "input_img": bf(np.random.standard_normal((B, D)) * s[D:D + D])[:, None, :],
        "input_compress": bf(np.random.standard_normal((B, C)) * s[D + D:]),
        "base_text_features": bf(np.random.standard_normal((B, N, H)) * rt),
        "base_img_features": bf(np.random.standard_normal((B, N, H)) * ri),
        "W_user": bf(np.random.standard_normal((H, F)) / np.sqrt(F) / s * t[:, None]),
        "b_user": bf(np.random.standard_normal(H) * 0.3 * t),
        "Wl_img": bf(np.random.standard_normal((O, H)) * 0.5 * np.sqrt(N / H) / ri),
        "bl_img": bf(np.random.standard_normal(O) * 0.2),
        "Wr_img": bf(np.random.standard_normal((O, H)) * 0.5 / np.sqrt(H) / t),
        "Wl_txt": bf(np.random.standard_normal((O, H)) * 0.5 * np.sqrt(N / H) / rt),
        "bl_txt": bf(np.random.standard_normal(O) * 0.2),
        "Wr_txt": bf(np.random.standard_normal((O, H)) * 0.5 / np.sqrt(H) / t),
    }


def reference(input_text, input_img, input_compress, base_text_features, base_img_features,
              W_user, b_user, Wl_img, bl_img, Wr_img, Wl_txt, bl_txt, Wr_txt):
    feat = np.concatenate([f64(input_text)[:, 0], f64(input_img)[:, 0], f64(input_compress)], axis=-1)
    u = (mxq(feat, 1, "e4m3") @ mxq(f64(W_user), 1, "e4m3").T) + f64(b_user)
    mean_img = f64(base_img_features).mean(axis=1)
    mean_txt = f64(base_text_features).mean(axis=1)
    uq = mxq(u, 1, "e4m3")
    out = ((mxq(mean_img, 1, "e4m3") @ mxq(f64(Wl_img), 1, "e4m3").T) + f64(bl_img)
           + (uq @ mxq(f64(Wr_img), 1, "e4m3").T)
           + (mxq(mean_txt, 1, "e4m3") @ mxq(f64(Wl_txt), 1, "e4m3").T) + f64(bl_txt)
           + (uq @ mxq(f64(Wr_txt), 1, "e4m3").T))
    return np.maximum(out, 0.0)

@@ -1,0 +1,288 @@
+from contextlib import ExitStack
+
+import concourse.mybir as mybir
+from concourse.masks import make_identity
+
+BF16 = mybir.dt.bfloat16
+F32 = mybir.dt.float32
+U32 = mybir.dt.uint32
+U8 = mybir.dt.uint8
+FP8X4 = mybir.dt.float8_e4m3fn_x4
+ADD = mybir.AluOpType.add
+IS_GE = mybir.AluOpType.is_ge
+RELU = mybir.ActivationFunctionType.Relu
+
+P = 128
+PACK = 4
+K_PASS = P * PACK
+
+USERS = 512
+NODES = 24
+WIDTH = 512
+FEAT_PASSES = 3
+USER_TILES = USERS // P
+
+LOAD_NODES = 8
+PAIRS = LOAD_NODES // 2
+USER_LOADS = NODES // LOAD_NODES
+ROW_TILES = 4
+
+PART_NODES = 3
+SPAN_USERS = P * PART_NODES // NODES
+LOAD_SPANS = 2
+
+FLOPS = 2 * USERS * WIDTH * (FEAT_PASSES * K_PASS + 4 * K_PASS) + 2 * USERS * NODES * WIDTH
+
+
+def mx_tiles(pool, name, passes, columns):
+    codes = pool.tile([P, passes, columns], U32, name=name + "_codes", align_bytes=64)
+    scales = pool.tile([P, passes, columns], U8, name=name + "_scales", align_bytes=64)
+    return codes, scales
+
+
+def quantise(nc, grouped, operand, k_pass, columns):
+    codes, scales = operand
+    nc.vector.quantize_mx(
+        out=codes[:, k_pass, columns].bitcast(FP8X4),
+        scales=scales[:, k_pass, columns],
+        in_=grouped.rearrange("p r t -> p (r t)"),
+    )
+
+
+def mx_pass(nc, acc, left, left_pass, left_columns, right, right_pass, right_columns, start, stop):
+    nc.tensor.matmul_mx(
+        out=acc,
+        lhsT=left[0][:, left_pass, left_columns].bitcast(FP8X4),
+        lhsT_scale=left[1][:, left_pass, left_columns],
+        rhs=right[0][:, right_pass, right_columns].bitcast(FP8X4),
+        rhs_scale=right[1][:, right_pass, right_columns],
+        start=start,
+        stop=stop,
+    )
+
+
+def tile_graphlearner_ib_pa_kernel(
+    tc,
+    input_text,
+    input_img,
+    input_compress,
+    base_text_features,
+    base_img_features,
+    W_user,
+    b_user,
+    Wl_img,
+    bl_img,
+    Wr_img,
+    Wl_txt,
+    bl_txt,
+    Wr_txt,
+    out,
+):
+    nc = tc.nc
+    with ExitStack() as ctx:
+        const = ctx.enter_context(tc.tile_pool(name="const", bufs=1))
+        keep = ctx.enter_context(tc.tile_pool(name="keep", bufs=1))
+        raw = ctx.enter_context(tc.tile_pool(name="raw", bufs=10))
+        stage = ctx.enter_context(tc.tile_pool(name="stage", bufs=3))
+        user_rows = ctx.enter_context(tc.tile_pool(name="user_rows", bufs=6))
+        pair_sums = ctx.enter_context(tc.tile_pool(name="pair_sums", bufs=4))
+        node_rows = ctx.enter_context(tc.tile_pool(name="node_rows", bufs=6))
+        results = ctx.enter_context(tc.tile_pool(name="results", bufs=2))
+        prep_banks = ctx.enter_context(tc.psum_pool(name="prep_banks", bufs=5))
+        sum_banks = ctx.enter_context(tc.psum_pool(name="sum_banks", bufs=2))
+        out_banks = ctx.enter_context(tc.psum_pool(name="out_banks", bufs=1))
+
+        b_user_bf16 = const.tile([P, PACK], BF16)
+        nc.sync.dma_start(out=b_user_bf16, in_=b_user.rearrange("(p t) -> p t", t=PACK))
+        b_user_columns = const.tile([P, PACK], F32)
+        nc.vector.tensor_copy(out=b_user_columns, in_=b_user_bf16)
+        bias_rows = const.tile([P, WIDTH], BF16)
+        nc.vector.memset(bias_rows, 0.0)
+        nc.sync.dma_start(out=bias_rows[0:1, :], in_=bl_img.rearrange("(o n) -> o n", o=1))
+        nc.sync.dma_start(out=bias_rows[1:2, :], in_=bl_txt.rearrange("(o n) -> o n", o=1))
+
+        identity = const.tile([P, P], BF16)
+        make_identity(nc, identity)
+        identity_f32 = const.tile([P, P], F32)
+        make_identity(nc, identity_f32)
+        ones = const.tile([P, P], BF16)
+        nc.vector.memset(ones, 1.0)
+
+        user_parts = P // SPAN_USERS
+        member_f32 = const.tile([P, SPAN_USERS], F32)
+        nc.gpsimd.memset(member_f32, 1.0)
+        nc.gpsimd.affine_select(
+            out=member_f32, in_=member_f32, pattern=[[-user_parts, SPAN_USERS]],
+            compare_op=IS_GE, fill=0.0, base=0, channel_multiplier=1,
+        )
+        nc.gpsimd.affine_select(
+            out=member_f32, in_=member_f32, pattern=[[user_parts, SPAN_USERS]],
+            compare_op=IS_GE, fill=0.0, base=user_parts - 1, channel_multiplier=-1,
+        )
+        member = const.tile([P, SPAN_USERS], BF16)
+        nc.vector.tensor_copy(out=member, in_=member_f32)
+
+        bias_bank = out_banks.tile([P, WIDTH], F32, name="acc")
+        nc.tensor.matmul(out=bias_bank, lhsT=ones, rhs=bias_rows, start=True, stop=True)
+        out_bias = const.tile([P, WIDTH], F32)
+        nc.vector.tensor_copy(out=out_bias, in_=bias_bank)
+
+        w_user_mx = mx_tiles(keep, "w_user", FEAT_PASSES, WIDTH)
+        feat_mx = mx_tiles(keep, "feat", FEAT_PASSES, USERS)
+        u_mx = mx_tiles(keep, "u", 1, USERS)
+        wr_img_mx = mx_tiles(keep, "wr_img", 1, WIDTH)
+        wr_txt_mx = mx_tiles(keep, "wr_txt", 1, WIDTH)
+        wl_img_mx = mx_tiles(keep, "wl_img", 1, WIDTH)
+        wl_txt_mx = mx_tiles(keep, "wl_txt", 1, WIDTH)
+        mean_mx = {"img": mx_tiles(keep, "mean_img", 1, USERS), "txt": mx_tiles(keep, "mean_txt", 1, USERS)}
+        u_grouped = keep.tile([P, USERS, PACK], BF16, align_bytes=64)
+
+        feat_parts = (input_text[:, 0, :], input_img[:, 0, :], input_compress)
+        pieces = []
+        for c in range(FEAT_PASSES):
+            pieces.append({"matrix": W_user[:, c * K_PASS : (c + 1) * K_PASS], "operand": w_user_mx, "k_pass": c, "rows": "(p j) k -> p j k"})
+            pieces.append({"matrix": feat_parts[c], "operand": feat_mx, "k_pass": c, "rows": "(j p) k -> p j k"})
+        for weight, operand in ((Wr_img, wr_img_mx), (Wr_txt, wr_txt_mx), (Wl_img, wl_img_mx), (Wl_txt, wl_txt_mx)):
+            pieces.append({"matrix": weight, "operand": operand, "k_pass": 0, "rows": "(j p) k -> p j k"})
+        pieces.append({"user_tiles": (0, 1)})
+        pieces.append({"user_tiles": (2, 3)})
+
+        def begin_piece(piece):
+            if "matrix" in piece:
+                rows = raw.tile([P, ROW_TILES, K_PASS], BF16, name="rows")
+                nc.sync.dma_start(out=rows, in_=piece["matrix"].rearrange(piece["rows"], p=P))
+                grouped = stage.tile([P, ROW_TILES * P, PACK], BF16, name="grouped", align_bytes=64)
+                for j in range(ROW_TILES):
+                    turned = prep_banks.tile([P, PACK, P], BF16, name="prep_bank")
+                    for t in range(PACK):
+                        nc.tensor.transpose(turned[:, t, :], rows[:, j, t:K_PASS:PACK], identity)
+                    nc.scalar.copy(out=grouped[:, j * P : (j + 1) * P, :], in_=turned.rearrange("p t r -> p r t"))
+                piece["grouped"] = grouped
+            else:
+                piece["banks"] = []
+                for ut in piece["user_tiles"]:
+                    u_bank = prep_banks.tile([P, PACK, P], F32, name="prep_bank")
+                    for t in range(PACK):
+                        for c in range(FEAT_PASSES):
+                            mx_pass(
+                                nc, u_bank[:, t, :], w_user_mx, c, slice(t * P, (t + 1) * P),
+                                feat_mx, c, slice(ut * P, (ut + 1) * P),
+                                start=(c == 0), stop=(c == FEAT_PASSES - 1),
+                            )
+                    piece["banks"].append(u_bank)
+
+        def end_piece(piece):
+            if "matrix" in piece:
+                quantise(nc, piece["grouped"], piece["operand"], piece["k_pass"], slice(0, ROW_TILES * P))
+            else:
+                for ut, u_bank in zip(piece["user_tiles"], piece["banks"]):
+                    nc.vector.tensor_tensor(
+                        out=u_grouped[:, ut * P : (ut + 1) * P, :],
+                        in0=u_bank.rearrange("p t b -> p b t"),
+                        in1=b_user_columns.unsqueeze(1).to_broadcast([P, P, PACK]),
+                        op=ADD,
+                    )
+                if piece["user_tiles"][-1] == USER_TILES - 1:
+                    quantise(nc, u_grouped, u_mx, 0, slice(0, USERS))
+
+        def add_users_load(base, ut, load, sum_bank):
+            nodes = user_rows.tile([P, LOAD_NODES, WIDTH], BF16, name="nodes")
+            nc.sync.dma_start(
+                out=nodes, in_=base[ut * P : (ut + 1) * P, load * LOAD_NODES : (load + 1) * LOAD_NODES, :]
+            )
+            pairs = pair_sums.tile([P, PAIRS, WIDTH], F32, name="pairs")
+            nc.vector.tensor_tensor(out=pairs, in0=nodes[:, 0:PAIRS, :], in1=nodes[:, PAIRS:LOAD_NODES, :], op=ADD)
+            for t in range(PACK):
+                for pair in range(PAIRS):
+                    nc.tensor.matmul(
+                        out=sum_bank[:, t, :],
+                        lhsT=pairs[:, pair, t:WIDTH:PACK],
+                        rhs=identity_f32,
+                        is_transpose=True,
+                        start=(load == 0 and t == 0 and pair == 0),
+                        stop=(load == USER_LOADS - 1 and t == PACK - 1 and pair == PAIRS - 1),
+                    )
+
+        def add_nodes_load(base, ut, load, sum_bank):
+            span_nodes = P * PART_NODES
+            first_node = ut * P * NODES + load * LOAD_SPANS * span_nodes
+            rows = node_rows.tile([P, LOAD_SPANS, PART_NODES, WIDTH], BF16, name="node_rows")
+            nc.sync.dma_start(
+                out=rows.rearrange("p s j h -> p s (j h)"),
+                in_=base.rearrange("b n h -> (b n) h")[
+                    first_node : first_node + LOAD_SPANS * span_nodes, :
+                ].rearrange("(s p j) h -> p s (j h)", p=P, j=PART_NODES),
+            )
+            for s in range(LOAD_SPANS):
+                first_user = (load * LOAD_SPANS + s) * SPAN_USERS
+                for t in range(PACK):
+                    for j in range(PART_NODES):
+                        nc.tensor.matmul(
+                            out=sum_bank[:, t, first_user : first_user + SPAN_USERS],
+                            lhsT=rows[:, s, j, t:WIDTH:PACK],
+                            rhs=member,
+                            start=(j == 0),
+                            stop=(j == PART_NODES - 1),
+                        )
+
+        def gather(block):
+            mean_grouped = stage.tile([P, P, PACK], BF16, name="mean_grouped", align_bytes=64)
+            nc.scalar.mul(out=mean_grouped, in_=block["sum_bank"].rearrange("p t b -> p b t"), mul=1.0 / NODES)
+            block["mean_grouped"] = mean_grouped
+
+        def multiply(block):
+            users = slice(block["ut"] * P, (block["ut"] + 1) * P)
+            quantise(nc, block["mean_grouped"], mean_mx[block["kind"]], 0, users)
+            if block["kind"] == "txt":
+                acc = out_banks.tile([P, WIDTH], F32, name="acc")
+                products = (
+                    (u_mx, wr_img_mx),
+                    (u_mx, wr_txt_mx),
+                    (mean_mx["img"], wl_img_mx),
+                    (mean_mx["txt"], wl_txt_mx),
+                )
+                for i, (left, right) in enumerate(products):
+                    mx_pass(
+                        nc, acc, left, 0, users, right, 0, slice(0, WIDTH),
+                        start=(i == 0), stop=(i == len(products) - 1),
+                    )
+                block["acc"] = acc
+
+        def store(block):
+            if block["kind"] == "txt":
+                biased = results.tile([P, WIDTH], F32, name="biased")
+                nc.vector.tensor_tensor(out=biased, in0=block["acc"], in1=out_bias, op=ADD)
+                result = results.tile([P, WIDTH], F32, name="result")
+                nc.scalar.activation(out=result, in_=biased, func=RELU)
+                nc.scalar.dma_start(out=out[block["ut"] * P : (block["ut"] + 1) * P, :], in_=result)
+
+        previous = None
+        begun = None
+        number = 0
+        for kind, base in (("img", base_img_features), ("txt", base_text_features)):
+            for ut in range(USER_TILES):
+                block = {"kind": kind, "ut": ut, "by_matmul": number >= 5}
+                number += 1
+                block["sum_bank"] = sum_banks.tile([P, PACK, P], F32, name="sum_bank")
+                loads = P // (LOAD_SPANS * SPAN_USERS) if block["by_matmul"] else USER_LOADS
+                for load in range(loads):
+                    piece = pieces.pop(0) if pieces else None
+                    if piece is not None:
+                        begin_piece(piece)
+                    if block["by_matmul"]:
+                        add_nodes_load(base, ut, load, block["sum_bank"])
+                    else:
+                        add_users_load(base, ut, load, block["sum_bank"])
+                    if begun is not None:
+                        end_piece(begun)
+                    begun = piece
+                    if previous is not None and load == 0:
+                        gather(previous)
+                    if previous is not None and load == 1:
+                        multiply(previous)
+                    if previous is not None and load == 2:
+                        store(previous)
+                previous = block
+        gather(previous)
+        multiply(previous)
+        store(previous)

@@ -30,6 +30,7 @@ ROW_TILES = 4
 PART_NODES = 3
 SPAN_USERS = P * PART_NODES // NODES
 LOAD_SPANS = 2
+NODE_LOADS = P // (LOAD_SPANS * SPAN_USERS)
 
 FLOPS = 2 * USERS * WIDTH * (FEAT_PASSES * K_PASS + 4 * K_PASS) + 2 * USERS * NODES * WIDTH
 
@@ -62,47 +63,31 @@ def mx_pass(nc, acc, left, left_pass, left_columns, right, right_pass, right_col
 
 
 def tile_graphlearner_ib_pa_kernel(
-    tc,
-    input_text,
-    input_img,
-    input_compress,
-    base_text_features,
-    base_img_features,
-    W_user,
-    b_user,
-    Wl_img,
-    bl_img,
-    Wr_img,
-    Wl_txt,
-    bl_txt,
-    Wr_txt,
-    out,
+    tc, input_text, input_img, input_compress, base_text_features, base_img_features,
+    W_user, b_user, Wl_img, bl_img, Wr_img, Wl_txt, bl_txt, Wr_txt, out,
 ):
     nc = tc.nc
     with ExitStack() as ctx:
         const = ctx.enter_context(tc.tile_pool(name="const", bufs=1))
         keep = ctx.enter_context(tc.tile_pool(name="keep", bufs=1))
-        raw = ctx.enter_context(tc.tile_pool(name="raw", bufs=10))
-        stage = ctx.enter_context(tc.tile_pool(name="stage", bufs=3))
+        raw = ctx.enter_context(tc.tile_pool(name="raw", bufs=6))
+        raw_user = ctx.enter_context(tc.tile_pool(name="raw_user", bufs=2))
+        stage = ctx.enter_context(tc.tile_pool(name="stage", bufs=4))
         user_rows = ctx.enter_context(tc.tile_pool(name="user_rows", bufs=6))
-        pair_sums = ctx.enter_context(tc.tile_pool(name="pair_sums", bufs=4))
-        node_rows = ctx.enter_context(tc.tile_pool(name="node_rows", bufs=6))
+        pair_sums = ctx.enter_context(tc.tile_pool(name="pair_sums", bufs=3))
+        node_rows = ctx.enter_context(tc.tile_pool(name="node_rows", bufs=7))
         results = ctx.enter_context(tc.tile_pool(name="results", bufs=2))
-        prep_banks = ctx.enter_context(tc.psum_pool(name="prep_banks", bufs=5))
-        sum_banks = ctx.enter_context(tc.psum_pool(name="sum_banks", bufs=2))
+        prep_banks = ctx.enter_context(tc.psum_pool(name="prep_banks", bufs=3))
+        sum_banks = ctx.enter_context(tc.psum_pool(name="sum_banks", bufs=4))
         out_banks = ctx.enter_context(tc.psum_pool(name="out_banks", bufs=1))
 
         b_user_bf16 = const.tile([P, PACK], BF16)
-        nc.sync.dma_start(out=b_user_bf16, in_=b_user.rearrange("(p t) -> p t", t=PACK))
-        b_user_columns = const.tile([P, PACK], F32)
-        nc.vector.tensor_copy(out=b_user_columns, in_=b_user_bf16)
+        nc.scalar.dma_start(out=b_user_bf16, in_=b_user.rearrange("(p t) -> p t", t=PACK))
         bias_rows = const.tile([P, WIDTH], BF16)
         nc.vector.memset(bias_rows, 0.0)
-        nc.sync.dma_start(out=bias_rows[0:1, :], in_=bl_img.rearrange("(o n) -> o n", o=1))
-        nc.sync.dma_start(out=bias_rows[1:2, :], in_=bl_txt.rearrange("(o n) -> o n", o=1))
+        nc.scalar.dma_start(out=bias_rows[0:1, :], in_=bl_img.rearrange("(o n) -> o n", o=1))
+        nc.scalar.dma_start(out=bias_rows[1:2, :], in_=bl_txt.rearrange("(o n) -> o n", o=1))
 
-        identity = const.tile([P, P], BF16)
-        make_identity(nc, identity)
         identity_f32 = const.tile([P, P], F32)
         make_identity(nc, identity_f32)
         ones = const.tile([P, P], BF16)
@@ -122,10 +107,8 @@ def tile_graphlearner_ib_pa_kernel(
         member = const.tile([P, SPAN_USERS], BF16)
         nc.vector.tensor_copy(out=member, in_=member_f32)
 
-        bias_bank = out_banks.tile([P, WIDTH], F32, name="acc")
-        nc.tensor.matmul(out=bias_bank, lhsT=ones, rhs=bias_rows, start=True, stop=True)
+        b_user_columns = const.tile([P, PACK], F32)
         out_bias = const.tile([P, WIDTH], F32)
-        nc.vector.tensor_copy(out=out_bias, in_=bias_bank)
 
         w_user_mx = mx_tiles(keep, "w_user", FEAT_PASSES, WIDTH)
         feat_mx = mx_tiles(keep, "feat", FEAT_PASSES, USERS)
@@ -137,79 +120,128 @@ def tile_graphlearner_ib_pa_kernel(
         mean_mx = {"img": mx_tiles(keep, "mean_img", 1, USERS), "txt": mx_tiles(keep, "mean_txt", 1, USERS)}
         u_grouped = keep.tile([P, USERS, PACK], BF16, align_bytes=64)
 
-        feat_parts = (input_text[:, 0, :], input_img[:, 0, :], input_compress)
-        pieces = []
-        for c in range(FEAT_PASSES):
-            pieces.append({"matrix": W_user[:, c * K_PASS : (c + 1) * K_PASS], "operand": w_user_mx, "k_pass": c, "rows": "(p j) k -> p j k"})
-            pieces.append({"matrix": feat_parts[c], "operand": feat_mx, "k_pass": c, "rows": "(j p) k -> p j k"})
-        for weight, operand in ((Wr_img, wr_img_mx), (Wr_txt, wr_txt_mx), (Wl_img, wl_img_mx), (Wl_txt, wl_txt_mx)):
-            pieces.append({"matrix": weight, "operand": operand, "k_pass": 0, "rows": "(j p) k -> p j k"})
-        pieces.append({"user_tiles": (0, 1)})
-        pieces.append({"user_tiles": (2, 3)})
-
-        def begin_piece(piece):
-            if "matrix" in piece:
-                rows = raw.tile([P, ROW_TILES, K_PASS], BF16, name="rows")
-                nc.sync.dma_start(out=rows, in_=piece["matrix"].rearrange(piece["rows"], p=P))
-                grouped = stage.tile([P, ROW_TILES * P, PACK], BF16, name="grouped", align_bytes=64)
-                for j in range(ROW_TILES):
-                    turned = prep_banks.tile([P, PACK, P], BF16, name="prep_bank")
-                    for t in range(PACK):
-                        nc.tensor.transpose(turned[:, t, :], rows[:, j, t:K_PASS:PACK], identity)
-                    nc.scalar.copy(out=grouped[:, j * P : (j + 1) * P, :], in_=turned.rearrange("p t r -> p r t"))
-                piece["grouped"] = grouped
-            else:
-                piece["banks"] = []
-                for ut in piece["user_tiles"]:
-                    u_bank = prep_banks.tile([P, PACK, P], F32, name="prep_bank")
-                    for t in range(PACK):
-                        for c in range(FEAT_PASSES):
-                            mx_pass(
-                                nc, u_bank[:, t, :], w_user_mx, c, slice(t * P, (t + 1) * P),
-                                feat_mx, c, slice(ut * P, (ut + 1) * P),
-                                start=(c == 0), stop=(c == FEAT_PASSES - 1),
-                            )
-                    piece["banks"].append(u_bank)
-
-        def end_piece(piece):
-            if "matrix" in piece:
-                quantise(nc, piece["grouped"], piece["operand"], piece["k_pass"], slice(0, ROW_TILES * P))
-            else:
-                for ut, u_bank in zip(piece["user_tiles"], piece["banks"]):
-                    nc.vector.tensor_tensor(
-                        out=u_grouped[:, ut * P : (ut + 1) * P, :],
-                        in0=u_bank.rearrange("p t b -> p b t"),
-                        in1=b_user_columns.unsqueeze(1).to_broadcast([P, P, PACK]),
-                        op=ADD,
+        def turn(words, first_word, grouped):
+            bank = prep_banks.tile([P, 2, 2, P], F32, name="prep_bank")
+            for j in range(2):
+                for half in range(2):
+                    nc.tensor.transpose(
+                        bank[:, j, half, :],
+                        words[:, j, first_word + half : first_word + K_PASS // 2 : 2],
+                        identity_f32,
                     )
-                if piece["user_tiles"][-1] == USER_TILES - 1:
-                    quantise(nc, u_grouped, u_mx, 0, slice(0, USERS))
+            nc.scalar.copy(
+                out=grouped.bitcast(F32).rearrange("p (j r) h -> p j r h", j=2),
+                in_=bank.rearrange("p j h r -> p j r h"),
+            )
 
-        def add_users_load(base, ut, load, sum_bank):
+        def begin_w_user(piece):
+            rows = raw_user.tile([P, 2, FEAT_PASSES * K_PASS], BF16, name="w_user_rows")
+            first = 2 * piece["half"]
+            nc.sync.dma_start(out=rows, in_=W_user.rearrange("(p j) k -> p j k", j=PACK)[:, first : first + 2, :])
+            piece["grouped"] = []
+            for c in range(FEAT_PASSES):
+                grouped = stage.tile([P, 2 * P, PACK], BF16, name="w_user_grouped", align_bytes=64)
+                turn(rows[:].bitcast(F32), c * K_PASS // 2, grouped[:])
+                piece["grouped"].append(grouped)
+
+        def end_w_user(piece):
+            columns = slice(piece["half"] * 2 * P, (piece["half"] + 1) * 2 * P)
+            for c in range(FEAT_PASSES):
+                quantise(nc, piece["grouped"][c], w_user_mx, c, columns)
+
+        def begin_matrix(piece):
+            rows = raw.tile([P, ROW_TILES, K_PASS], BF16, name="rows")
+            nc.sync.dma_start(out=rows, in_=piece["matrix"].rearrange(piece["order"], p=P))
+            grouped = stage.tile([P, ROW_TILES * P, PACK], BF16, name="grouped", align_bytes=64)
+            for pair in range(ROW_TILES // 2):
+                turn(
+                    rows[:, 2 * pair : 2 * pair + 2, :].bitcast(F32), 0,
+                    grouped[:, 2 * pair * P : (2 * pair + 2) * P, :],
+                )
+            piece["grouped"] = grouped
+
+        def end_matrix(piece):
+            quantise(nc, piece["grouped"], piece["operand"], piece["k_pass"], slice(0, ROW_TILES * P))
+
+        def begin_u(piece):
+            ut = piece["ut"]
+            u_bank = prep_banks.tile([P, PACK, P], F32, name="prep_bank")
+            for t in range(PACK):
+                for c in range(FEAT_PASSES):
+                    mx_pass(
+                        nc, u_bank[:, t, :], w_user_mx, c, slice(t * P, (t + 1) * P),
+                        feat_mx, c, slice(ut * P, (ut + 1) * P),
+                        start=(c == 0), stop=(c == FEAT_PASSES - 1),
+                    )
+            piece["bank"] = u_bank
+
+        def end_u(piece):
+            ut = piece["ut"]
+            nc.vector.tensor_tensor(
+                out=u_grouped[:, ut * P : (ut + 1) * P, :],
+                in0=piece["bank"].rearrange("p t b -> p b t"),
+                in1=b_user_columns.unsqueeze(1).to_broadcast([P, P, PACK]),
+                op=ADD,
+            )
+            if ut == USER_TILES - 1:
+                quantise(nc, u_grouped, u_mx, 0, slice(0, USERS))
+
+        def begin_biases(piece):
+            piece["bank"] = out_banks.tile([P, ROW_TILES, P], F32, name="acc")
+            nc.tensor.matmul(
+                out=piece["bank"].rearrange("p j r -> p (j r)"), lhsT=ones, rhs=bias_rows, start=True, stop=True
+            )
+
+        def end_biases(piece):
+            nc.vector.tensor_copy(out=out_bias, in_=piece["bank"].rearrange("p j r -> p (j r)"))
+            nc.vector.tensor_copy(out=b_user_columns, in_=b_user_bf16)
+
+        pieces = [{"begin": begin_w_user, "end": end_w_user, "half": half} for half in range(2)]
+        for c, part in enumerate((input_text[:, 0, :], input_img[:, 0, :], input_compress)):
+            pieces.append({"begin": begin_matrix, "end": end_matrix, "matrix": part, "order": "(j p) k -> p j k",
+                           "operand": feat_mx, "k_pass": c})
+        weights = []
+        for weight, operand in ((Wr_img, wr_img_mx), (Wr_txt, wr_txt_mx), (Wl_img, wl_img_mx), (Wl_txt, wl_txt_mx)):
+            weights.append({"begin": begin_matrix, "end": end_matrix, "matrix": weight, "order": "(p j) k -> p j k",
+                            "operand": operand, "k_pass": 0})
+        pieces += weights
+        pieces.append({"begin": begin_biases, "end": end_biases})
+        pieces += [{"begin": begin_u, "end": end_u, "ut": ut} for ut in range(USER_TILES)]
+
+        bases = {"img": base_img_features, "txt": base_text_features}
+
+        def add_users_load(block, load):
+            ut = block["ut"]
             nodes = user_rows.tile([P, LOAD_NODES, WIDTH], BF16, name="nodes")
             nc.sync.dma_start(
-                out=nodes, in_=base[ut * P : (ut + 1) * P, load * LOAD_NODES : (load + 1) * LOAD_NODES, :]
+                out=nodes,
+                in_=bases[block["kind"]][ut * P : (ut + 1) * P, load * LOAD_NODES : (load + 1) * LOAD_NODES, :],
             )
-            pairs = pair_sums.tile([P, PAIRS, WIDTH], F32, name="pairs")
-            nc.vector.tensor_tensor(out=pairs, in0=nodes[:, 0:PAIRS, :], in1=nodes[:, PAIRS:LOAD_NODES, :], op=ADD)
+            pairs = pair_sums.tile([P, PAIRS, PACK, P], F32, name="pairs")
+            nc.vector.tensor_tensor(
+                out=pairs,
+                in0=nodes[:, 0:PAIRS, :].rearrange("p n (q t) -> p n t q", t=PACK),
+                in1=nodes[:, PAIRS:LOAD_NODES, :].rearrange("p n (q t) -> p n t q", t=PACK),
+                op=ADD,
+            )
             for t in range(PACK):
                 for pair in range(PAIRS):
                     nc.tensor.matmul(
-                        out=sum_bank[:, t, :],
-                        lhsT=pairs[:, pair, t:WIDTH:PACK],
+                        out=block["sum_bank"][:, t, :],
+                        lhsT=pairs[:, pair, t, :],
                         rhs=identity_f32,
                         is_transpose=True,
                         start=(load == 0 and t == 0 and pair == 0),
                         stop=(load == USER_LOADS - 1 and t == PACK - 1 and pair == PAIRS - 1),
                     )
 
-        def add_nodes_load(base, ut, load, sum_bank):
+        def add_nodes_load(block, load):
             span_nodes = P * PART_NODES
-            first_node = ut * P * NODES + load * LOAD_SPANS * span_nodes
+            first_node = block["ut"] * P * NODES + load * LOAD_SPANS * span_nodes
             rows = node_rows.tile([P, LOAD_SPANS, PART_NODES, WIDTH], BF16, name="node_rows")
             nc.sync.dma_start(
                 out=rows.rearrange("p s j h -> p s (j h)"),
-                in_=base.rearrange("b n h -> (b n) h")[
+                in_=bases[block["kind"]].rearrange("b n h -> (b n) h")[
                     first_node : first_node + LOAD_SPANS * span_nodes, :
                 ].rearrange("(s p j) h -> p s (j h)", p=P, j=PART_NODES),
             )
@@ -218,71 +250,107 @@ def tile_graphlearner_ib_pa_kernel(
                 for t in range(PACK):
                     for j in range(PART_NODES):
                         nc.tensor.matmul(
-                            out=sum_bank[:, t, first_user : first_user + SPAN_USERS],
+                            out=block["sum_bank"][:, t, first_user : first_user + SPAN_USERS],
                             lhsT=rows[:, s, j, t:WIDTH:PACK],
                             rhs=member,
                             start=(j == 0),
                             stop=(j == PART_NODES - 1),
                         )
 
+        done = []
+
         def gather(block):
             mean_grouped = stage.tile([P, P, PACK], BF16, name="mean_grouped", align_bytes=64)
             nc.scalar.mul(out=mean_grouped, in_=block["sum_bank"].rearrange("p t b -> p b t"), mul=1.0 / NODES)
             block["mean_grouped"] = mean_grouped
 
-        def multiply(block):
+        def quantise_mean(block):
             users = slice(block["ut"] * P, (block["ut"] + 1) * P)
             quantise(nc, block["mean_grouped"], mean_mx[block["kind"]], 0, users)
-            if block["kind"] == "txt":
-                acc = out_banks.tile([P, WIDTH], F32, name="acc")
-                products = (
-                    (u_mx, wr_img_mx),
-                    (u_mx, wr_txt_mx),
-                    (mean_mx["img"], wl_img_mx),
-                    (mean_mx["txt"], wl_txt_mx),
+            done.append((block["kind"], block["ut"]))
+
+        def multiply(tile):
+            users = slice(tile["ut"] * P, (tile["ut"] + 1) * P)
+            acc = out_banks.tile([P, ROW_TILES, P], F32, name="acc")
+            products = (
+                (u_mx, wr_img_mx),
+                (u_mx, wr_txt_mx),
+                (mean_mx["img"], wl_img_mx),
+                (mean_mx["txt"], wl_txt_mx),
+            )
+            for i, (left, right) in enumerate(products):
+                mx_pass(
+                    nc, acc.rearrange("p j r -> p (j r)"), left, 0, users, right, 0, slice(0, WIDTH),
+                    start=(i == 0), stop=(i == len(products) - 1),
                 )
-                for i, (left, right) in enumerate(products):
-                    mx_pass(
-                        nc, acc, left, 0, users, right, 0, slice(0, WIDTH),
-                        start=(i == 0), stop=(i == len(products) - 1),
-                    )
-                block["acc"] = acc
+            tile["acc"] = acc
 
-        def store(block):
-            if block["kind"] == "txt":
-                biased = results.tile([P, WIDTH], F32, name="biased")
-                nc.vector.tensor_tensor(out=biased, in0=block["acc"], in1=out_bias, op=ADD)
-                result = results.tile([P, WIDTH], F32, name="result")
-                nc.scalar.activation(out=result, in_=biased, func=RELU)
-                nc.scalar.dma_start(out=out[block["ut"] * P : (block["ut"] + 1) * P, :], in_=result)
+        def store(tile):
+            ut = tile["ut"]
+            biased = results.tile([P, P, ROW_TILES], F32, name="biased")
+            nc.vector.tensor_tensor(
+                out=biased, in0=tile["acc"].rearrange("p j r -> p r j"),
+                in1=out_bias.rearrange("p (r j) -> p r j", j=ROW_TILES), op=ADD,
+            )
+            result = results.tile([P, WIDTH], F32, name="result")
+            nc.scalar.activation(out=result, in_=biased.rearrange("p r j -> p (r j)"), func=RELU)
+            nc.scalar.dma_start(out=out[ut * P : (ut + 1) * P, :], in_=result)
 
-        previous = None
+        user_blocks = (("img", 0), ("txt", 0), ("img", 1), ("img", 2), ("img", 3))
+        node_blocks = (("txt", 1), ("txt", 2), ("txt", 3))
+
+        def block_loads(blocks, add_load, loads):
+            queue = []
+            for kind, ut in blocks:
+                block = {"kind": kind, "ut": ut, "add_load": add_load, "loads": loads}
+                queue += [(block, load) for load in range(loads)]
+            return queue
+
+        user_queue = block_loads(user_blocks, add_users_load, USER_LOADS)
+        node_queue = block_loads(node_blocks, add_nodes_load, NODE_LOADS)
+        order = []
+        node_at = 0
+        for i, entry in enumerate(user_queue):
+            order.append(entry)
+            while node_at * len(user_queue) < (i - 2) * len(node_queue):
+                order.append(node_queue[node_at])
+                node_at += 1
+        order += node_queue[node_at:]
+
+        waiting = []
+        multiplied = set()
         begun = None
-        number = 0
-        for kind, base in (("img", base_img_features), ("txt", base_text_features)):
+        u_ready = False
+
+        def write_waiting():
+            for steps in list(waiting):
+                steps.pop(0)()
+                if not steps:
+                    waiting.remove(steps)
+
+        def write_tiles():
             for ut in range(USER_TILES):
-                block = {"kind": kind, "ut": ut, "by_matmul": number >= 5}
-                number += 1
+                if u_ready and ut not in multiplied and ("img", ut) in done and ("txt", ut) in done:
+                    multiplied.add(ut)
+                    tile = {"ut": ut}
+                    multiply(tile)
+                    waiting.append([lambda tile=tile: store(tile)])
+
+        for block, load in order:
+            piece = pieces.pop(0) if pieces else None
+            if piece is not None:
+                piece["begin"](piece)
+            if load == 0:
                 block["sum_bank"] = sum_banks.tile([P, PACK, P], F32, name="sum_bank")
-                loads = P // (LOAD_SPANS * SPAN_USERS) if block["by_matmul"] else USER_LOADS
-                for load in range(loads):
-                    piece = pieces.pop(0) if pieces else None
-                    if piece is not None:
-                        begin_piece(piece)
-                    if block["by_matmul"]:
-                        add_nodes_load(base, ut, load, block["sum_bank"])
-                    else:
-                        add_users_load(base, ut, load, block["sum_bank"])
-                    if begun is not None:
-                        end_piece(begun)
-                    begun = piece
-                    if previous is not None and load == 0:
-                        gather(previous)
-                    if previous is not None and load == 1:
-                        multiply(previous)
-                    if previous is not None and load == 2:
-                        store(previous)
-                previous = block
-        gather(previous)
-        multiply(previous)
-        store(previous)
+            block["add_load"](block, load)
+            if begun is not None:
+                begun["end"](begun)
+                u_ready = u_ready or begun.get("ut") == USER_TILES - 1
+            begun = piece
+            write_waiting()
+            write_tiles()
+            if load == block["loads"] - 1:
+                waiting.append([lambda block=block: gather(block), lambda block=block: quantise_mean(block)])
+        while waiting:
+            write_waiting()
+            write_tiles()

@@ -82,11 +82,11 @@ def tile_graphlearner_ib_pa_kernel(
         out_banks = ctx.enter_context(tc.psum_pool(name="out_banks", bufs=1))
 
         b_user_bf16 = const.tile([P, PACK], BF16)
-        nc.scalar.dma_start(out=b_user_bf16, in_=b_user.rearrange("(p t) -> p t", t=PACK))
+        nc.sync.dma_start(out=b_user_bf16, in_=b_user.rearrange("(p t) -> p t", t=PACK))
         bias_rows = const.tile([P, WIDTH], BF16)
         nc.vector.memset(bias_rows, 0.0)
-        nc.scalar.dma_start(out=bias_rows[0:1, :], in_=bl_img.rearrange("(o n) -> o n", o=1))
-        nc.scalar.dma_start(out=bias_rows[1:2, :], in_=bl_txt.rearrange("(o n) -> o n", o=1))
+        nc.sync.dma_start(out=bias_rows[0:1, :], in_=bl_img.rearrange("(o n) -> o n", o=1))
+        nc.sync.dma_start(out=bias_rows[1:2, :], in_=bl_txt.rearrange("(o n) -> o n", o=1))
 
         identity_f32 = const.tile([P, P], F32)
         make_identity(nc, identity_f32)
@@ -208,6 +208,7 @@ def tile_graphlearner_ib_pa_kernel(
         pieces.append({"begin": begin_biases, "end": end_biases})
         pieces += [{"begin": begin_u, "end": end_u, "ut": ut} for ut in range(USER_TILES)]
 
+        late = []
         bases = {"img": base_img_features, "txt": base_text_features}
 
         def add_users_load(block, load):
@@ -224,6 +225,9 @@ def tile_graphlearner_ib_pa_kernel(
                 in1=nodes[:, PAIRS:LOAD_NODES, :].rearrange("p n (q t) -> p n t q", t=PACK),
                 op=ADD,
             )
+            late.append(lambda: turn_pairs(block, load, pairs))
+
+        def turn_pairs(block, load, pairs):
             for t in range(PACK):
                 for pair in range(PAIRS):
                     nc.tensor.matmul(
@@ -296,6 +300,7 @@ def tile_graphlearner_ib_pa_kernel(
             nc.scalar.activation(out=result, in_=biased.rearrange("p r j -> p (r j)"), func=RELU)
             nc.scalar.dma_start(out=out[ut * P : (ut + 1) * P, :], in_=result)
 
+        ctx.enter_context(tc.manual_schedule(engines={mybir.EngineType.PE}))
         user_blocks = (("img", 0), ("txt", 0), ("img", 1), ("img", 2), ("img", 3))
         node_blocks = (("txt", 1), ("txt", 2), ("txt", 3))
 
@@ -342,7 +347,11 @@ def tile_graphlearner_ib_pa_kernel(
                 piece["begin"](piece)
             if load == 0:
                 block["sum_bank"] = sum_banks.tile([P, PACK, P], F32, name="sum_bank")
+            before = list(late)
+            late.clear()
             block["add_load"](block, load)
+            for step in before:
+                step()
             if begun is not None:
                 begun["end"](begun)
                 u_ready = u_ready or begun.get("ut") == USER_TILES - 1
@@ -351,6 +360,8 @@ def tile_graphlearner_ib_pa_kernel(
             write_tiles()
             if load == block["loads"] - 1:
                 waiting.append([lambda block=block: gather(block), lambda block=block: quantise_mean(block)])
+        for step in late:
+            step()
         while waiting:
             write_waiting()
             write_tiles()

@@ -32,6 +32,8 @@ SPAN_USERS = P * PART_NODES // NODES
 LOAD_SPANS = 2
 NODE_LOADS = P // (LOAD_SPANS * SPAN_USERS)
 
+FOLDED_LOADS = (0, 1)
+
 FLOPS = 2 * USERS * WIDTH * (FEAT_PASSES * K_PASS + 4 * K_PASS) + 2 * USERS * NODES * WIDTH
 
 
@@ -225,18 +227,28 @@ def tile_graphlearner_ib_pa_kernel(
                 in1=nodes[:, PAIRS:LOAD_NODES, :].rearrange("p n (q t) -> p n t q", t=PACK),
                 op=ADD,
             )
-            late.append(lambda: turn_pairs(block, load, pairs))
+            if load in FOLDED_LOADS:
+                late.append(lambda: fold_pairs(block, load, pairs))
+            else:
+                late.append(lambda: turn_sums(block, load, pairs, PAIRS))
 
-        def turn_pairs(block, load, pairs):
+        def fold_pairs(block, load, pairs):
+            fours = pair_sums.tile([P, PAIRS // 2, PACK, P], F32, name="fours")
+            nc.vector.tensor_tensor(
+                out=fours, in0=pairs[:, 0 : PAIRS // 2], in1=pairs[:, PAIRS // 2 : PAIRS], op=ADD
+            )
+            turn_sums(block, load, fours, PAIRS // 2)
+
+        def turn_sums(block, load, sums, count):
             for t in range(PACK):
-                for pair in range(PAIRS):
+                for i in range(count):
                     nc.tensor.matmul(
                         out=block["sum_bank"][:, t, :],
-                        lhsT=pairs[:, pair, t, :],
+                        lhsT=sums[:, i, t, :],
                         rhs=identity_f32,
                         is_transpose=True,
-                        start=(load == 0 and t == 0 and pair == 0),
-                        stop=(load == USER_LOADS - 1 and t == PACK - 1 and pair == PAIRS - 1),
+                        start=(load == 0 and t == 0 and i == 0),
+                        stop=(load == USER_LOADS - 1 and t == PACK - 1 and i == count - 1),
                     )
 
         def add_nodes_load(block, load):

@@ -27,12 +27,10 @@ PAIRS = LOAD_NODES // 2
 USER_LOADS = NODES // LOAD_NODES
 ROW_TILES = 4
 
-PART_NODES = 3
-SPAN_USERS = P * PART_NODES // NODES
-LOAD_SPANS = 2
-NODE_LOADS = P // (LOAD_SPANS * SPAN_USERS)
+LOAD_USERS = 32
+NODE_LOADS = P // LOAD_USERS
 
-FOLDED_LOADS = (0, 1)
+FOLDED_LOADS = ()
 
 FLOPS = 2 * USERS * WIDTH * (FEAT_PASSES * K_PASS + 4 * K_PASS) + 2 * USERS * NODES * WIDTH
 
@@ -85,32 +83,41 @@ def tile_graphlearner_ib_pa_kernel(
 
         b_user_bf16 = const.tile([P, PACK], BF16)
         nc.sync.dma_start(out=b_user_bf16, in_=b_user.rearrange("(p t) -> p t", t=PACK))
-        bias_rows = const.tile([P, WIDTH], BF16)
-        nc.vector.memset(bias_rows, 0.0)
-        nc.sync.dma_start(out=bias_rows[0:1, :], in_=bl_img.rearrange("(o n) -> o n", o=1))
-        nc.sync.dma_start(out=bias_rows[1:2, :], in_=bl_txt.rearrange("(o n) -> o n", o=1))
+        bl_img_bf16 = const.tile([P, PACK], BF16)
+        nc.sync.dma_start(out=bl_img_bf16, in_=bl_img.rearrange("(p t) -> p t", t=PACK))
+        bl_txt_bf16 = const.tile([P, PACK], BF16)
+        nc.sync.dma_start(out=bl_txt_bf16, in_=bl_txt.rearrange("(p t) -> p t", t=PACK))
 
         identity_f32 = const.tile([P, P], F32)
         make_identity(nc, identity_f32)
-        ones = const.tile([P, P], BF16)
-        nc.vector.memset(ones, 1.0)
+        zeros_f32 = const.tile([P, P], F32)
+        nc.vector.memset(zeros_f32, 0.0)
 
-        user_parts = P // SPAN_USERS
-        member_f32 = const.tile([P, SPAN_USERS], F32)
-        nc.gpsimd.memset(member_f32, 1.0)
-        nc.gpsimd.affine_select(
-            out=member_f32, in_=member_f32, pattern=[[-user_parts, SPAN_USERS]],
-            compare_op=IS_GE, fill=0.0, base=0, channel_multiplier=1,
-        )
-        nc.gpsimd.affine_select(
-            out=member_f32, in_=member_f32, pattern=[[user_parts, SPAN_USERS]],
-            compare_op=IS_GE, fill=0.0, base=user_parts - 1, channel_multiplier=-1,
-        )
-        member = const.tile([P, SPAN_USERS], BF16)
-        nc.vector.tensor_copy(out=member, in_=member_f32)
+        members = {}
+        for part_nodes in (2, 3):
+            user_parts = NODES // part_nodes
+            members[part_nodes] = []
+            for s in range(1 if part_nodes == 3 else LOAD_USERS * user_parts // P):
+                first = s * P // user_parts
+                count = (s * P + P - 1) // user_parts - first + 1
+                offset = s * P - first * user_parts
+                member_f32 = const.tile([P, count], F32, name=f"member_f32_{part_nodes}_{s}")
+                nc.gpsimd.memset(member_f32, 1.0)
+                nc.gpsimd.affine_select(
+                    out=member_f32, in_=member_f32, pattern=[[-user_parts, count]],
+                    compare_op=IS_GE, fill=0.0, base=offset, channel_multiplier=1,
+                )
+                nc.gpsimd.affine_select(
+                    out=member_f32, in_=member_f32, pattern=[[user_parts, count]],
+                    compare_op=IS_GE, fill=0.0, base=user_parts - 1 - offset, channel_multiplier=-1,
+                )
+                member = const.tile([P, count], BF16, name=f"member_{part_nodes}_{s}")
+                nc.vector.tensor_copy(out=member, in_=member_f32)
+                members[part_nodes].append((first, count, member))
 
         b_user_columns = const.tile([P, PACK], F32)
-        out_bias = const.tile([P, WIDTH], F32)
+        bias_columns = const.tile([P, PACK], F32)
+        out_bias = const.tile([P, PACK, P], F32)
 
         w_user_mx = mx_tiles(keep, "w_user", FEAT_PASSES, WIDTH)
         feat_mx = mx_tiles(keep, "feat", FEAT_PASSES, USERS)
@@ -189,14 +196,16 @@ def tile_graphlearner_ib_pa_kernel(
                 quantise(nc, u_grouped, u_mx, 0, slice(0, USERS))
 
         def begin_biases(piece):
+            nc.vector.tensor_copy(out=b_user_columns, in_=b_user_bf16)
+            nc.vector.tensor_tensor(out=bias_columns, in0=bl_img_bf16, in1=bl_txt_bf16, op=ADD)
             piece["bank"] = out_banks.tile([P, ROW_TILES, P], F32, name="acc")
-            nc.tensor.matmul(
-                out=piece["bank"].rearrange("p j r -> p (j r)"), lhsT=ones, rhs=bias_rows, start=True, stop=True
-            )
+            for j in range(PACK):
+                nc.tensor.transpose(
+                    piece["bank"][:, j, :], bias_columns[:, j : j + 1].to_broadcast([P, P]), identity_f32
+                )
 
         def end_biases(piece):
-            nc.vector.tensor_copy(out=out_bias, in_=piece["bank"].rearrange("p j r -> p (j r)"))
-            nc.vector.tensor_copy(out=b_user_columns, in_=b_user_bf16)
+            nc.vector.tensor_copy(out=out_bias, in_=piece["bank"])
 
         pieces = [{"begin": begin_w_user, "end": end_w_user, "half": half} for half in range(2)]
         for c, part in enumerate((input_text[:, 0, :], input_img[:, 0, :], input_compress)):
@@ -252,25 +261,35 @@ def tile_graphlearner_ib_pa_kernel(
                     )
 
         def add_nodes_load(block, load):
-            span_nodes = P * PART_NODES
-            first_node = block["ut"] * P * NODES + load * LOAD_SPANS * span_nodes
-            rows = node_rows.tile([P, LOAD_SPANS, PART_NODES, WIDTH], BF16, name="node_rows")
+            part_nodes = block["part_nodes"]
+            spans = LOAD_USERS * NODES // (P * part_nodes)
+            first_node = (block["ut"] * P + load * LOAD_USERS) * NODES
+            rows = node_rows.tile([P, spans, part_nodes, WIDTH], BF16, name="node_rows")
             nc.sync.dma_start(
                 out=rows.rearrange("p s j h -> p s (j h)"),
                 in_=bases[block["kind"]].rearrange("b n h -> (b n) h")[
-                    first_node : first_node + LOAD_SPANS * span_nodes, :
-                ].rearrange("(s p j) h -> p s (j h)", p=P, j=PART_NODES),
+                    first_node : first_node + LOAD_USERS * NODES, :
+                ].rearrange("(s p j) h -> p s (j h)", p=P, j=part_nodes),
             )
-            for s in range(LOAD_SPANS):
-                first_user = (load * LOAD_SPANS + s) * SPAN_USERS
+            shared = part_nodes == 2
+            if shared and load == 0:
                 for t in range(PACK):
-                    for j in range(PART_NODES):
+                    nc.tensor.matmul(
+                        out=block["sum_bank"][:, t, :], lhsT=zeros_f32, rhs=identity_f32,
+                        is_transpose=True, start=(t == 0), stop=False,
+                    )
+            for s in range(spans):
+                first, count, member = members[part_nodes][s if shared else 0]
+                first_user = load * LOAD_USERS + (first if shared else s * count)
+                for t in range(PACK):
+                    for j in range(part_nodes):
+                        last = load == NODE_LOADS - 1 and s == spans - 1 and t == PACK - 1
                         nc.tensor.matmul(
-                            out=block["sum_bank"][:, t, first_user : first_user + SPAN_USERS],
+                            out=block["sum_bank"][:, t, first_user : first_user + count],
                             lhsT=rows[:, s, j, t:WIDTH:PACK],
                             rhs=member,
-                            start=(j == 0),
-                            stop=(j == PART_NODES - 1),
+                            start=(j == 0 and not shared),
+                            stop=(j == part_nodes - 1 and (last or not shared)),
                         )
 
         done = []
@@ -306,20 +325,20 @@ def tile_graphlearner_ib_pa_kernel(
             biased = results.tile([P, P, ROW_TILES], F32, name="biased")
             nc.vector.tensor_tensor(
                 out=biased, in0=tile["acc"].rearrange("p j r -> p r j"),
-                in1=out_bias.rearrange("p (r j) -> p r j", j=ROW_TILES), op=ADD,
+                in1=out_bias.rearrange("p j r -> p r j"), op=ADD,
             )
             result = results.tile([P, WIDTH], F32, name="result")
             nc.scalar.activation(out=result, in_=biased.rearrange("p r j -> p (r j)"), func=RELU)
-            nc.scalar.dma_start(out=out[ut * P : (ut + 1) * P, :], in_=result)
+            queue = nc.scalar if ut == USER_TILES - 1 else nc.gpsimd
+            queue.dma_start(out=out[ut * P : (ut + 1) * P, :], in_=result)
 
-        ctx.enter_context(tc.manual_schedule(engines={mybir.EngineType.PE}))
-        user_blocks = (("img", 0), ("txt", 0), ("img", 1), ("img", 2), ("img", 3))
-        node_blocks = (("txt", 1), ("txt", 2), ("txt", 3))
+        user_blocks = [("img", ut, None) for ut in range(USER_TILES)]
+        node_blocks = [("txt", ut, 2 if ut < 2 else 3) for ut in range(USER_TILES)]
 
         def block_loads(blocks, add_load, loads):
             queue = []
-            for kind, ut in blocks:
-                block = {"kind": kind, "ut": ut, "add_load": add_load, "loads": loads}
+            for kind, ut, part_nodes in blocks:
+                block = {"kind": kind, "ut": ut, "part_nodes": part_nodes, "add_load": add_load, "loads": loads}
                 queue += [(block, load) for load in range(loads)]
             return queue
 
@@ -329,7 +348,7 @@ def tile_graphlearner_ib_pa_kernel(
         node_at = 0
         for i, entry in enumerate(user_queue):
             order.append(entry)
-            while node_at * len(user_queue) < (i - 2) * len(node_queue):
+            while node_at * len(user_queue) < (i - 1) * len(node_queue):
                 order.append(node_queue[node_at])
                 node_at += 1
         order += node_queue[node_at:]

@@ -27,10 +27,11 @@ PAIRS = LOAD_NODES // 2
 USER_LOADS = NODES // LOAD_NODES
 ROW_TILES = 4
 
-LOAD_USERS = 32
-NODE_LOADS = P // LOAD_USERS
-
-FOLDED_LOADS = ()
+PART_NODES = 3
+SPAN_USERS = P * PART_NODES // NODES
+SPANS = P // SPAN_USERS
+LOAD_SPANS = 2
+LAST_USERS = 32
 
 FLOPS = 2 * USERS * WIDTH * (FEAT_PASSES * K_PASS + 4 * K_PASS) + 2 * USERS * NODES * WIDTH
 
@@ -70,50 +71,34 @@ def tile_graphlearner_ib_pa_kernel(
     with ExitStack() as ctx:
         const = ctx.enter_context(tc.tile_pool(name="const", bufs=1))
         keep = ctx.enter_context(tc.tile_pool(name="keep", bufs=1))
-        raw = ctx.enter_context(tc.tile_pool(name="raw", bufs=6))
-        raw_user = ctx.enter_context(tc.tile_pool(name="raw_user", bufs=2))
-        stage = ctx.enter_context(tc.tile_pool(name="stage", bufs=4))
-        user_rows = ctx.enter_context(tc.tile_pool(name="user_rows", bufs=6))
+        loads = ctx.enter_context(tc.tile_pool(name="loads", bufs=17))
+        stage = ctx.enter_context(tc.tile_pool(name="stage", bufs=3))
         pair_sums = ctx.enter_context(tc.tile_pool(name="pair_sums", bufs=3))
-        node_rows = ctx.enter_context(tc.tile_pool(name="node_rows", bufs=7))
         results = ctx.enter_context(tc.tile_pool(name="results", bufs=2))
         prep_banks = ctx.enter_context(tc.psum_pool(name="prep_banks", bufs=3))
         sum_banks = ctx.enter_context(tc.psum_pool(name="sum_banks", bufs=4))
         out_banks = ctx.enter_context(tc.psum_pool(name="out_banks", bufs=1))
 
-        b_user_bf16 = const.tile([P, PACK], BF16)
-        nc.sync.dma_start(out=b_user_bf16, in_=b_user.rearrange("(p t) -> p t", t=PACK))
-        bl_img_bf16 = const.tile([P, PACK], BF16)
-        nc.sync.dma_start(out=bl_img_bf16, in_=bl_img.rearrange("(p t) -> p t", t=PACK))
-        bl_txt_bf16 = const.tile([P, PACK], BF16)
-        nc.sync.dma_start(out=bl_txt_bf16, in_=bl_txt.rearrange("(p t) -> p t", t=PACK))
+        bias_rows = const.tile([P, WIDTH], BF16)
+        nc.vector.memset(bias_rows, 0.0)
+        identity = const.tile([P, P], BF16)
+        make_identity(nc, identity)
 
         identity_f32 = const.tile([P, P], F32)
         make_identity(nc, identity_f32)
-        zeros_f32 = const.tile([P, P], F32)
-        nc.vector.memset(zeros_f32, 0.0)
-
-        members = {}
-        for part_nodes in (2, 3):
-            user_parts = NODES // part_nodes
-            members[part_nodes] = []
-            for s in range(1 if part_nodes == 3 else LOAD_USERS * user_parts // P):
-                first = s * P // user_parts
-                count = (s * P + P - 1) // user_parts - first + 1
-                offset = s * P - first * user_parts
-                member_f32 = const.tile([P, count], F32, name=f"member_f32_{part_nodes}_{s}")
-                nc.gpsimd.memset(member_f32, 1.0)
-                nc.gpsimd.affine_select(
-                    out=member_f32, in_=member_f32, pattern=[[-user_parts, count]],
-                    compare_op=IS_GE, fill=0.0, base=offset, channel_multiplier=1,
-                )
-                nc.gpsimd.affine_select(
-                    out=member_f32, in_=member_f32, pattern=[[user_parts, count]],
-                    compare_op=IS_GE, fill=0.0, base=user_parts - 1 - offset, channel_multiplier=-1,
-                )
-                member = const.tile([P, count], BF16, name=f"member_{part_nodes}_{s}")
-                nc.vector.tensor_copy(out=member, in_=member_f32)
-                members[part_nodes].append((first, count, member))
+        user_parts = P // SPAN_USERS
+        member_f32 = const.tile([P, SPAN_USERS], F32)
+        nc.gpsimd.memset(member_f32, 1.0)
+        nc.gpsimd.affine_select(
+            out=member_f32, in_=member_f32, pattern=[[-user_parts, SPAN_USERS]],
+            compare_op=IS_GE, fill=0.0, base=0, channel_multiplier=1,
+        )
+        nc.gpsimd.affine_select(
+            out=member_f32, in_=member_f32, pattern=[[user_parts, SPAN_USERS]],
+            compare_op=IS_GE, fill=0.0, base=user_parts - 1, channel_multiplier=-1,
+        )
+        member = const.tile([P, SPAN_USERS], BF16)
+        nc.vector.tensor_copy(out=member, in_=member_f32)
 
         b_user_columns = const.tile([P, PACK], F32)
         bias_columns = const.tile([P, PACK], F32)
@@ -144,7 +129,7 @@ def tile_graphlearner_ib_pa_kernel(
             )
 
         def begin_w_user(piece):
-            rows = raw_user.tile([P, 2, FEAT_PASSES * K_PASS], BF16, name="w_user_rows")
+            rows = loads.tile([P, 2, FEAT_PASSES * K_PASS], BF16, name="load")
             first = 2 * piece["half"]
             nc.sync.dma_start(out=rows, in_=W_user.rearrange("(p j) k -> p j k", j=PACK)[:, first : first + 2, :])
             piece["grouped"] = []
@@ -159,8 +144,8 @@ def tile_graphlearner_ib_pa_kernel(
                 quantise(nc, piece["grouped"][c], w_user_mx, c, columns)
 
         def begin_matrix(piece):
-            rows = raw.tile([P, ROW_TILES, K_PASS], BF16, name="rows")
-            nc.sync.dma_start(out=rows, in_=piece["matrix"].rearrange(piece["order"], p=P))
+            rows = loads.tile([P, ROW_TILES, K_PASS], BF16, name="load")
+            nc.sync.dma_start(out=rows, in_=piece["matrix"].rearrange("(p j) k -> p j k", p=P))
             grouped = stage.tile([P, ROW_TILES * P, PACK], BF16, name="grouped", align_bytes=64)
             for pair in range(ROW_TILES // 2):
                 turn(
@@ -187,7 +172,7 @@ def tile_graphlearner_ib_pa_kernel(
         def end_u(piece):
             ut = piece["ut"]
             nc.vector.tensor_tensor(
-                out=u_grouped[:, ut * P : (ut + 1) * P, :],
+                out=u_grouped.rearrange("p (b j) t -> p j b t", j=ROW_TILES)[:, ut],
                 in0=piece["bank"].rearrange("p t b -> p b t"),
                 in1=b_user_columns.unsqueeze(1).to_broadcast([P, P, PACK]),
                 op=ADD,
@@ -195,28 +180,40 @@ def tile_graphlearner_ib_pa_kernel(
             if ut == USER_TILES - 1:
                 quantise(nc, u_grouped, u_mx, 0, slice(0, USERS))
 
-        def begin_biases(piece):
-            nc.vector.tensor_copy(out=b_user_columns, in_=b_user_bf16)
-            nc.vector.tensor_tensor(out=bias_columns, in0=bl_img_bf16, in1=bl_txt_bf16, op=ADD)
+        def load_biases(piece):
+            for row, vector in enumerate((b_user, bl_img, bl_txt)):
+                nc.sync.dma_start(out=bias_rows[row : row + 1, :], in_=vector.rearrange("(o n) -> o n", o=1))
+
+        def turn_biases(piece):
+            turned = prep_banks.tile([P, PACK, P], BF16, name="prep_bank")
+            for t in range(PACK):
+                nc.tensor.transpose(turned[:, t, :], bias_rows[:, t:WIDTH:PACK], identity)
+            bias_parts = const.tile([P, 3, PACK], F32)
+            nc.vector.tensor_copy(out=bias_parts, in_=turned[:, :, 0:3].rearrange("p t v -> p v t"))
+            nc.vector.tensor_copy(out=b_user_columns, in_=bias_parts[:, 0, :])
+            nc.vector.tensor_tensor(out=bias_columns, in0=bias_parts[:, 1, :], in1=bias_parts[:, 2, :], op=ADD)
+
+        def begin_spread(piece):
             piece["bank"] = out_banks.tile([P, ROW_TILES, P], F32, name="acc")
             for j in range(PACK):
                 nc.tensor.transpose(
                     piece["bank"][:, j, :], bias_columns[:, j : j + 1].to_broadcast([P, P]), identity_f32
                 )
 
-        def end_biases(piece):
+        def end_spread(piece):
             nc.vector.tensor_copy(out=out_bias, in_=piece["bank"])
 
         pieces = [{"begin": begin_w_user, "end": end_w_user, "half": half} for half in range(2)]
         for c, part in enumerate((input_text[:, 0, :], input_img[:, 0, :], input_compress)):
-            pieces.append({"begin": begin_matrix, "end": end_matrix, "matrix": part, "order": "(j p) k -> p j k",
+            pieces.append({"begin": begin_matrix, "end": end_matrix, "matrix": part,
                            "operand": feat_mx, "k_pass": c})
         weights = []
         for weight, operand in ((Wr_img, wr_img_mx), (Wr_txt, wr_txt_mx), (Wl_img, wl_img_mx), (Wl_txt, wl_txt_mx)):
-            weights.append({"begin": begin_matrix, "end": end_matrix, "matrix": weight, "order": "(p j) k -> p j k",
+            weights.append({"begin": begin_matrix, "end": end_matrix, "matrix": weight,
                             "operand": operand, "k_pass": 0})
         pieces += weights
-        pieces.append({"begin": begin_biases, "end": end_biases})
+        pieces.insert(5, {"begin": load_biases, "end": turn_biases})
+        pieces.append({"begin": begin_spread, "end": end_spread})
         pieces += [{"begin": begin_u, "end": end_u, "ut": ut} for ut in range(USER_TILES)]
 
         late = []
@@ -224,7 +221,7 @@ def tile_graphlearner_ib_pa_kernel(
 
         def add_users_load(block, load):
             ut = block["ut"]
-            nodes = user_rows.tile([P, LOAD_NODES, WIDTH], BF16, name="nodes")
+            nodes = loads.tile([P, LOAD_NODES, WIDTH], BF16, name="load")
             nc.sync.dma_start(
                 out=nodes,
                 in_=bases[block["kind"]][ut * P : (ut + 1) * P, load * LOAD_NODES : (load + 1) * LOAD_NODES, :],
@@ -236,17 +233,7 @@ def tile_graphlearner_ib_pa_kernel(
                 in1=nodes[:, PAIRS:LOAD_NODES, :].rearrange("p n (q t) -> p n t q", t=PACK),
                 op=ADD,
             )
-            if load in FOLDED_LOADS:
-                late.append(lambda: fold_pairs(block, load, pairs))
-            else:
-                late.append(lambda: turn_sums(block, load, pairs, PAIRS))
-
-        def fold_pairs(block, load, pairs):
-            fours = pair_sums.tile([P, PAIRS // 2, PACK, P], F32, name="fours")
-            nc.vector.tensor_tensor(
-                out=fours, in0=pairs[:, 0 : PAIRS // 2], in1=pairs[:, PAIRS // 2 : PAIRS], op=ADD
-            )
-            turn_sums(block, load, fours, PAIRS // 2)
+            late.append(lambda: turn_sums(block, load, pairs, PAIRS))
 
         def turn_sums(block, load, sums, count):
             for t in range(PACK):
@@ -260,44 +247,47 @@ def tile_graphlearner_ib_pa_kernel(
                         stop=(load == USER_LOADS - 1 and t == PACK - 1 and i == count - 1),
                     )
 
-        def add_nodes_load(block, load):
-            part_nodes = block["part_nodes"]
-            spans = LOAD_USERS * NODES // (P * part_nodes)
-            first_node = (block["ut"] * P + load * LOAD_USERS) * NODES
-            rows = node_rows.tile([P, spans, part_nodes, WIDTH], BF16, name="node_rows")
+        def add_nodes_load(block, spans):
+            span_nodes = P * PART_NODES
+            first_node = block["ut"] * P * NODES + spans.start * span_nodes
+            rows = loads.tile([P, len(spans), PART_NODES, WIDTH], BF16, name="load")
             nc.sync.dma_start(
                 out=rows.rearrange("p s j h -> p s (j h)"),
                 in_=bases[block["kind"]].rearrange("b n h -> (b n) h")[
-                    first_node : first_node + LOAD_USERS * NODES, :
-                ].rearrange("(s p j) h -> p s (j h)", p=P, j=part_nodes),
+                    first_node : first_node + len(spans) * span_nodes, :
+                ].rearrange("(s p j) h -> p s (j h)", p=P, j=PART_NODES),
             )
-            shared = part_nodes == 2
-            if shared and load == 0:
+            for s, span in enumerate(spans):
+                first_user = span * SPAN_USERS
+                bank = block["sum_bank"]
+                if first_user >= block["split"]:
+                    bank, first_user = block["last_bank"], first_user - block["split"]
                 for t in range(PACK):
-                    nc.tensor.matmul(
-                        out=block["sum_bank"][:, t, :], lhsT=zeros_f32, rhs=identity_f32,
-                        is_transpose=True, start=(t == 0), stop=False,
-                    )
-            for s in range(spans):
-                first, count, member = members[part_nodes][s if shared else 0]
-                first_user = load * LOAD_USERS + (first if shared else s * count)
-                for t in range(PACK):
-                    for j in range(part_nodes):
-                        last = load == NODE_LOADS - 1 and s == spans - 1 and t == PACK - 1
+                    for j in range(PART_NODES):
                         nc.tensor.matmul(
-                            out=block["sum_bank"][:, t, first_user : first_user + count],
+                            out=bank[:, t, first_user : first_user + SPAN_USERS],
                             lhsT=rows[:, s, j, t:WIDTH:PACK],
                             rhs=member,
-                            start=(j == 0 and not shared),
-                            stop=(j == part_nodes - 1 and (last or not shared)),
+                            start=(j == 0),
+                            stop=(j == PART_NODES - 1),
                         )
 
         done = []
 
         def gather(block):
-            mean_grouped = stage.tile([P, P, PACK], BF16, name="mean_grouped", align_bytes=64)
-            nc.scalar.mul(out=mean_grouped, in_=block["sum_bank"].rearrange("p t b -> p b t"), mul=1.0 / NODES)
-            block["mean_grouped"] = mean_grouped
+            block["mean_grouped"] = stage.tile([P, P, PACK], BF16, name="mean_grouped", align_bytes=64)
+            nc.scalar.mul(
+                out=block["mean_grouped"][:, 0 : block["split"], :],
+                in_=block["sum_bank"][:, :, 0 : block["split"]].rearrange("p t b -> p b t"),
+                mul=1.0 / NODES,
+            )
+
+        def gather_last(block):
+            nc.scalar.mul(
+                out=block["mean_grouped"][:, block["split"] : P, :],
+                in_=block["last_bank"][:, :, 0 : P - block["split"]].rearrange("p t b -> p b t"),
+                mul=1.0 / NODES,
+            )
 
         def quantise_mean(block):
             users = slice(block["ut"] * P, (block["ut"] + 1) * P)
@@ -322,33 +312,40 @@ def tile_graphlearner_ib_pa_kernel(
 
         def store(tile):
             ut = tile["ut"]
-            biased = results.tile([P, P, ROW_TILES], F32, name="biased")
-            nc.vector.tensor_tensor(
-                out=biased, in0=tile["acc"].rearrange("p j r -> p r j"),
-                in1=out_bias.rearrange("p j r -> p r j"), op=ADD,
-            )
-            result = results.tile([P, WIDTH], F32, name="result")
-            nc.scalar.activation(out=result, in_=biased.rearrange("p r j -> p (r j)"), func=RELU)
-            queue = nc.scalar if ut == USER_TILES - 1 else nc.gpsimd
-            queue.dma_start(out=out[ut * P : (ut + 1) * P, :], in_=result)
+            last = ut == USER_TILES - 1
+            parts = 2 if last else 1
+            for part in range(parts):
+                rows = slice(part * P // parts, (part + 1) * P // parts)
+                columns = slice(part * WIDTH // parts, (part + 1) * WIDTH // parts)
+                biased = results.tile([P, P // parts, ROW_TILES], F32, name="biased")
+                nc.vector.tensor_tensor(
+                    out=biased, in0=tile["acc"][:, :, rows].rearrange("p j r -> p r j"),
+                    in1=out_bias[:, :, rows].rearrange("p j r -> p r j"), op=ADD,
+                )
+                result = results.tile([P, WIDTH // parts], F32, name="result")
+                nc.scalar.activation(out=result, in_=biased.rearrange("p r j -> p (r j)"), func=RELU)
+                nc.scalar.dma_start(out=out[ut * P : (ut + 1) * P, columns], in_=result)
 
-        user_blocks = [("img", ut, None) for ut in range(USER_TILES)]
-        node_blocks = [("txt", ut, 2 if ut < 2 else 3) for ut in range(USER_TILES)]
-
-        def block_loads(blocks, add_load, loads):
-            queue = []
-            for kind, ut, part_nodes in blocks:
-                block = {"kind": kind, "ut": ut, "part_nodes": part_nodes, "add_load": add_load, "loads": loads}
-                queue += [(block, load) for load in range(loads)]
-            return queue
-
-        user_queue = block_loads(user_blocks, add_users_load, USER_LOADS)
-        node_queue = block_loads(node_blocks, add_nodes_load, NODE_LOADS)
+        ctx.enter_context(tc.manual_schedule(engines={mybir.EngineType.PE}))
+        user_blocks = (("img", 0), ("txt", 0), ("img", 1), ("img", 2), ("img", 3))
+        node_blocks = (("txt", 1), ("txt", 2), ("txt", 3))
+        user_queue, node_queue = [], []
+        for kind, ut in user_blocks:
+            block = {"kind": kind, "ut": ut, "split": P, "add_load": add_users_load}
+            user_queue += [(block, load, load == 0, load == USER_LOADS - 1) for load in range(USER_LOADS)]
+        for kind, ut in node_blocks:
+            last = (kind, ut) == node_blocks[-1]
+            block = {"kind": kind, "ut": ut, "split": P - LAST_USERS if last else P, "add_load": add_nodes_load}
+            starts = list(range(0, SPANS, LOAD_SPANS))
+            if last:
+                starts.append(SPANS - 1)
+            for first, end in zip(starts, starts[1:] + [SPANS]):
+                node_queue.append((block, range(first, end), first == 0, end == SPANS))
         order = []
         node_at = 0
         for i, entry in enumerate(user_queue):
             order.append(entry)
-            while node_at * len(user_queue) < (i - 1) * len(node_queue):
+            while node_at * len(user_queue) < (i - 2) * len(node_queue):
                 order.append(node_queue[node_at])
                 node_at += 1
         order += node_queue[node_at:]
@@ -372,12 +369,14 @@ def tile_graphlearner_ib_pa_kernel(
                     multiply(tile)
                     waiting.append([lambda tile=tile: store(tile)])
 
-        for block, load in order:
+        for block, load, first_load, last_load in order:
             piece = pieces.pop(0) if pieces else None
             if piece is not None:
                 piece["begin"](piece)
-            if load == 0:
+            if first_load:
                 block["sum_bank"] = sum_banks.tile([P, PACK, P], F32, name="sum_bank")
+                if block["split"] < P:
+                    block["last_bank"] = sum_banks.tile([P, PACK, P], F32, name="sum_bank")
             before = list(late)
             late.clear()
             block["add_load"](block, load)
@@ -389,8 +388,11 @@ def tile_graphlearner_ib_pa_kernel(
             begun = piece
             write_waiting()
             write_tiles()
-            if load == block["loads"] - 1:
-                waiting.append([lambda block=block: gather(block), lambda block=block: quantise_mean(block)])
+            if block["split"] < P and not last_load and load.stop * SPAN_USERS == block["split"]:
+                waiting.append([lambda block=block: gather(block)])
+            if last_load:
+                first_step = gather if block["split"] == P else gather_last
+                waiting.append([lambda block=block, step=first_step: step(block), lambda block=block: quantise_mean(block)])
         for step in late:
             step()
         while waiting:

@@ -27,11 +27,12 @@ PAIRS = LOAD_NODES // 2
 USER_LOADS = NODES // LOAD_NODES
 ROW_TILES = 4
 
-PART_NODES = 3
-SPAN_USERS = P * PART_NODES // NODES
-SPANS = P // SPAN_USERS
-LOAD_SPANS = 2
+LOAD_USERS = 32
 LAST_USERS = 32
+
+TURN_LAG = 1
+USER_LEAD = 4
+FOLDED_BLOCKS = 3
 
 FLOPS = 2 * USERS * WIDTH * (FEAT_PASSES * K_PASS + 4 * K_PASS) + 2 * USERS * NODES * WIDTH
 
@@ -71,8 +72,11 @@ def tile_graphlearner_ib_pa_kernel(
     with ExitStack() as ctx:
         const = ctx.enter_context(tc.tile_pool(name="const", bufs=1))
         keep = ctx.enter_context(tc.tile_pool(name="keep", bufs=1))
-        loads = ctx.enter_context(tc.tile_pool(name="loads", bufs=17))
+        user_rows = ctx.enter_context(tc.tile_pool(name="user_rows", bufs=6))
+        loads = ctx.enter_context(tc.tile_pool(name="loads", bufs=9))
         stage = ctx.enter_context(tc.tile_pool(name="stage", bufs=3))
+        w_user_stage = ctx.enter_context(tc.tile_pool(name="w_user_stage", bufs=2 * FEAT_PASSES))
+        four_sums = ctx.enter_context(tc.tile_pool(name="four_sums", bufs=5))
         pair_sums = ctx.enter_context(tc.tile_pool(name="pair_sums", bufs=3))
         results = ctx.enter_context(tc.tile_pool(name="results", bufs=2))
         prep_banks = ctx.enter_context(tc.psum_pool(name="prep_banks", bufs=3))
@@ -86,19 +90,30 @@ def tile_graphlearner_ib_pa_kernel(
 
         identity_f32 = const.tile([P, P], F32)
         make_identity(nc, identity_f32)
-        user_parts = P // SPAN_USERS
-        member_f32 = const.tile([P, SPAN_USERS], F32)
-        nc.gpsimd.memset(member_f32, 1.0)
-        nc.gpsimd.affine_select(
-            out=member_f32, in_=member_f32, pattern=[[-user_parts, SPAN_USERS]],
-            compare_op=IS_GE, fill=0.0, base=0, channel_multiplier=1,
-        )
-        nc.gpsimd.affine_select(
-            out=member_f32, in_=member_f32, pattern=[[user_parts, SPAN_USERS]],
-            compare_op=IS_GE, fill=0.0, base=user_parts - 1, channel_multiplier=-1,
-        )
-        member = const.tile([P, SPAN_USERS], BF16)
-        nc.vector.tensor_copy(out=member, in_=member_f32)
+        zeros_f32 = const.tile([P, P], F32)
+        nc.vector.memset(zeros_f32, 0.0)
+
+        members = {}
+        for part_nodes in (2, 3):
+            user_parts = NODES // part_nodes
+            members[part_nodes] = []
+            for s in range(1 if part_nodes == 3 else LOAD_USERS * user_parts // P):
+                first = s * P // user_parts
+                count = (s * P + P - 1) // user_parts - first + 1
+                offset = s * P - first * user_parts
+                member_f32 = const.tile([P, count], F32, name=f"member_f32_{part_nodes}_{s}")
+                nc.gpsimd.memset(member_f32, 1.0)
+                nc.gpsimd.affine_select(
+                    out=member_f32, in_=member_f32, pattern=[[-user_parts, count]],
+                    compare_op=IS_GE, fill=0.0, base=offset, channel_multiplier=1,
+                )
+                nc.gpsimd.affine_select(
+                    out=member_f32, in_=member_f32, pattern=[[user_parts, count]],
+                    compare_op=IS_GE, fill=0.0, base=user_parts - 1 - offset, channel_multiplier=-1,
+                )
+                member = const.tile([P, count], BF16, name=f"member_{part_nodes}_{s}")
+                nc.vector.tensor_copy(out=member, in_=member_f32)
+                members[part_nodes].append((first, count, member))
 
         b_user_columns = const.tile([P, PACK], F32)
         bias_columns = const.tile([P, PACK], F32)
@@ -134,7 +149,7 @@ def tile_graphlearner_ib_pa_kernel(
             nc.sync.dma_start(out=rows, in_=W_user.rearrange("(p j) k -> p j k", j=PACK)[:, first : first + 2, :])
             piece["grouped"] = []
             for c in range(FEAT_PASSES):
-                grouped = stage.tile([P, 2 * P, PACK], BF16, name="w_user_grouped", align_bytes=64)
+                grouped = w_user_stage.tile([P, 2 * P, PACK], BF16, name="w_user_grouped", align_bytes=64)
                 turn(rows[:].bitcast(F32), c * K_PASS // 2, grouped[:])
                 piece["grouped"].append(grouped)
 
@@ -221,7 +236,7 @@ def tile_graphlearner_ib_pa_kernel(
 
         def add_users_load(block, load):
             ut = block["ut"]
-            nodes = loads.tile([P, LOAD_NODES, WIDTH], BF16, name="load")
+            nodes = user_rows.tile([P, LOAD_NODES, WIDTH], BF16, name="nodes")
             nc.sync.dma_start(
                 out=nodes,
                 in_=bases[block["kind"]][ut * P : (ut + 1) * P, load * LOAD_NODES : (load + 1) * LOAD_NODES, :],
@@ -233,7 +248,17 @@ def tile_graphlearner_ib_pa_kernel(
                 in1=nodes[:, PAIRS:LOAD_NODES, :].rearrange("p n (q t) -> p n t q", t=PACK),
                 op=ADD,
             )
-            late.append(lambda: turn_sums(block, load, pairs, PAIRS))
+            if ut < FOLDED_BLOCKS:
+                late.append([lambda: fold_pairs(block, load, pairs)])
+            else:
+                late.append([lambda: None, lambda: turn_sums(block, load, pairs, PAIRS)])
+
+        def fold_pairs(block, load, pairs):
+            fours = four_sums.tile([P, PAIRS // 2, PACK, P], F32, name="fours")
+            nc.vector.tensor_tensor(
+                out=fours, in0=pairs[:, 0 : PAIRS // 2], in1=pairs[:, PAIRS // 2 : PAIRS], op=ADD
+            )
+            late.append([lambda: None] * TURN_LAG + [lambda: turn_sums(block, load, fours, PAIRS // 2)])
 
         def turn_sums(block, load, sums, count):
             for t in range(PACK):
@@ -246,33 +271,77 @@ def tile_graphlearner_ib_pa_kernel(
                         start=(load == 0 and t == 0 and i == 0),
                         stop=(load == USER_LOADS - 1 and t == PACK - 1 and i == count - 1),
                     )
+            if load == USER_LOADS - 1:
+                waiting.append(finish_steps(block))
 
-        def add_nodes_load(block, spans):
-            span_nodes = P * PART_NODES
-            first_node = block["ut"] * P * NODES + spans.start * span_nodes
-            rows = loads.tile([P, len(spans), PART_NODES, WIDTH], BF16, name="load")
+        def add_nodes_load(block, users):
+            part_nodes = block["part_nodes"]
+            spans = len(users) * NODES // (P * part_nodes)
+            first_node = (block["ut"] * P + users.start) * NODES
+            rows = loads.tile([P, spans, part_nodes, WIDTH], BF16, name="load")
             nc.sync.dma_start(
                 out=rows.rearrange("p s j h -> p s (j h)"),
                 in_=bases[block["kind"]].rearrange("b n h -> (b n) h")[
-                    first_node : first_node + len(spans) * span_nodes, :
-                ].rearrange("(s p j) h -> p s (j h)", p=P, j=PART_NODES),
+                    first_node : first_node + len(users) * NODES, :
+                ].rearrange("(s p j) h -> p s (j h)", p=P, j=part_nodes),
             )
-            for s, span in enumerate(spans):
-                first_user = span * SPAN_USERS
+            shared = part_nodes == 2
+            if shared and users.start == 0:
+                for t in range(PACK):
+                    nc.tensor.matmul(
+                        out=block["sum_bank"][:, t, :], lhsT=zeros_f32, rhs=identity_f32,
+                        is_transpose=True, start=(t == 0), stop=False,
+                    )
+            for s in range(spans):
+                first, count, member = members[part_nodes][s if shared else 0]
+                first_user = users.start + (first if shared else s * count)
                 bank = block["sum_bank"]
                 if first_user >= block["split"]:
                     bank, first_user = block["last_bank"], first_user - block["split"]
                 for t in range(PACK):
-                    for j in range(PART_NODES):
+                    features = slice(t, WIDTH, PACK) if block["direct"] else slice(t * P, (t + 1) * P)
+                    for j in range(part_nodes):
+                        last = users.stop == P and s == spans - 1 and t == PACK - 1
                         nc.tensor.matmul(
-                            out=bank[:, t, first_user : first_user + SPAN_USERS],
-                            lhsT=rows[:, s, j, t:WIDTH:PACK],
+                            out=bank[:, t, first_user : first_user + count],
+                            lhsT=rows[:, s, j, features],
                             rhs=member,
-                            start=(j == 0),
-                            stop=(j == PART_NODES - 1),
+                            start=(j == 0 and not shared),
+                            stop=(j == part_nodes - 1 and (last or not shared)),
                         )
 
         done = []
+
+        def round_means(block):
+            block["means"] = stage.tile([P, PACK, P], BF16, name="means", align_bytes=64)
+            nc.scalar.mul(out=block["means"], in_=block["sum_bank"], mul=1.0 / NODES)
+
+        def turn_back(block):
+            block["back"] = prep_banks.tile([P, WIDTH], BF16, name="prep_bank")
+            for t in range(PACK):
+                nc.tensor.transpose(block["back"][:, t * P : (t + 1) * P], block["means"][:, t, :], identity)
+
+        def permute(block):
+            block["mean_rows"] = stage.tile([P, PACK, P], BF16, name="mean_rows", align_bytes=64)
+            nc.vector.tensor_copy(out=block["mean_rows"], in_=block["back"].rearrange("p (q t) -> p t q", t=PACK))
+
+        def turn_forth(block):
+            block["forth"] = prep_banks.tile([P, PACK, P], BF16, name="prep_bank")
+            for t in range(PACK):
+                nc.tensor.transpose(block["forth"][:, t, :], block["mean_rows"][:, t, :], identity)
+
+        def group_means(block):
+            block["mean_grouped"] = stage.tile([P, P, PACK], BF16, name="mean_grouped", align_bytes=64)
+            nc.scalar.copy(out=block["mean_grouped"], in_=block["forth"].rearrange("p t b -> p b t"))
+
+        def finish_steps(block):
+            if block["split"] < P:
+                steps = [gather_last, quantise_mean]
+            elif block["direct"]:
+                steps = [gather, quantise_mean]
+            else:
+                steps = [round_means, turn_back, permute, turn_forth, group_means, quantise_mean]
+            return [lambda step=step: step(block) for step in steps]
 
         def gather(block):
             block["mean_grouped"] = stage.tile([P, P, PACK], BF16, name="mean_grouped", align_bytes=64)
@@ -327,25 +396,26 @@ def tile_graphlearner_ib_pa_kernel(
                 nc.scalar.dma_start(out=out[ut * P : (ut + 1) * P, columns], in_=result)
 
         ctx.enter_context(tc.manual_schedule(engines={mybir.EngineType.PE}))
-        user_blocks = (("img", 0), ("txt", 0), ("img", 1), ("img", 2), ("img", 3))
-        node_blocks = (("txt", 1), ("txt", 2), ("txt", 3))
         user_queue, node_queue = [], []
-        for kind, ut in user_blocks:
-            block = {"kind": kind, "ut": ut, "split": P, "add_load": add_users_load}
+        for ut in range(USER_TILES):
+            block = {"kind": "img", "ut": ut, "split": P, "direct": True, "add_load": add_users_load}
             user_queue += [(block, load, load == 0, load == USER_LOADS - 1) for load in range(USER_LOADS)]
-        for kind, ut in node_blocks:
-            last = (kind, ut) == node_blocks[-1]
-            block = {"kind": kind, "ut": ut, "split": P - LAST_USERS if last else P, "add_load": add_nodes_load}
-            starts = list(range(0, SPANS, LOAD_SPANS))
+        for ut in range(USER_TILES):
+            last = ut == USER_TILES - 1
+            block = {
+                "kind": "txt", "ut": ut, "part_nodes": 2 if ut < 2 else 3, "direct": last,
+                "split": P - LAST_USERS if last else P, "add_load": add_nodes_load,
+            }
+            starts = list(range(0, P, LOAD_USERS))
             if last:
-                starts.append(SPANS - 1)
-            for first, end in zip(starts, starts[1:] + [SPANS]):
-                node_queue.append((block, range(first, end), first == 0, end == SPANS))
+                starts.append(P - LOAD_USERS // 2)
+            for first, end in zip(starts, starts[1:] + [P]):
+                node_queue.append((block, range(first, end), first == 0, end == P))
         order = []
         node_at = 0
         for i, entry in enumerate(user_queue):
             order.append(entry)
-            while node_at * len(user_queue) < (i - 2) * len(node_queue):
+            while node_at * len(user_queue) < (i - USER_LEAD) * len(node_queue):
                 order.append(node_queue[node_at])
                 node_at += 1
         order += node_queue[node_at:]
@@ -355,11 +425,10 @@ def tile_graphlearner_ib_pa_kernel(
         begun = None
         u_ready = False
 
-        def write_waiting():
-            for steps in list(waiting):
+        def write_steps(lists):
+            for steps in list(lists):
                 steps.pop(0)()
-                if not steps:
-                    waiting.remove(steps)
+            lists[:] = [steps for steps in lists if steps]
 
         def write_tiles():
             for ut in range(USER_TILES):
@@ -380,21 +449,26 @@ def tile_graphlearner_ib_pa_kernel(
             before = list(late)
             late.clear()
             block["add_load"](block, load)
-            for step in before:
-                step()
+            for steps in before:
+                steps.pop(0)()
+                if steps:
+                    late.append(steps)
             if begun is not None:
                 begun["end"](begun)
                 u_ready = u_ready or begun.get("ut") == USER_TILES - 1
             begun = piece
-            write_waiting()
+            write_steps(waiting)
             write_tiles()
-            if block["split"] < P and not last_load and load.stop * SPAN_USERS == block["split"]:
+            if block["split"] < P and not last_load and load.stop == block["split"]:
                 waiting.append([lambda block=block: gather(block)])
-            if last_load:
-                first_step = gather if block["split"] == P else gather_last
-                waiting.append([lambda block=block, step=first_step: step(block), lambda block=block: quantise_mean(block)])
-        for step in late:
-            step()
-        while waiting:
-            write_waiting()
+            if last_load and block["kind"] == "txt":
+                waiting.append(finish_steps(block))
+        while late or waiting:
+            before = list(late)
+            late.clear()
+            for steps in before:
+                steps.pop(0)()
+                if steps:
+                    late.append(steps)
+            write_steps(waiting)
             write_tiles()

@@ -30,9 +30,10 @@ ROW_TILES = 4
 LOAD_USERS = 32
 LAST_USERS = 32
 
-TURN_LAG = 1
-USER_LEAD = 4
-FOLDED_BLOCKS = 3
+TURN_LAG = 2
+TILE_LAG = 1
+USER_LEAD = 3
+FOLDED_TWICE = 2
 
 FLOPS = 2 * USERS * WIDTH * (FEAT_PASSES * K_PASS + 4 * K_PASS) + 2 * USERS * NODES * WIDTH
 
@@ -160,7 +161,7 @@ def tile_graphlearner_ib_pa_kernel(
 
         def begin_matrix(piece):
             rows = loads.tile([P, ROW_TILES, K_PASS], BF16, name="load")
-            nc.sync.dma_start(out=rows, in_=piece["matrix"].rearrange("(p j) k -> p j k", p=P))
+            nc.sync.dma_start(out=rows, in_=piece["matrix"].rearrange(piece["order"], p=P))
             grouped = stage.tile([P, ROW_TILES * P, PACK], BF16, name="grouped", align_bytes=64)
             for pair in range(ROW_TILES // 2):
                 turn(
@@ -187,7 +188,7 @@ def tile_graphlearner_ib_pa_kernel(
         def end_u(piece):
             ut = piece["ut"]
             nc.vector.tensor_tensor(
-                out=u_grouped.rearrange("p (b j) t -> p j b t", j=ROW_TILES)[:, ut],
+                out=u_grouped[:, ut * P : (ut + 1) * P, :],
                 in0=piece["bank"].rearrange("p t b -> p b t"),
                 in1=b_user_columns.unsqueeze(1).to_broadcast([P, P, PACK]),
                 op=ADD,
@@ -220,11 +221,11 @@ def tile_graphlearner_ib_pa_kernel(
 
         pieces = [{"begin": begin_w_user, "end": end_w_user, "half": half} for half in range(2)]
         for c, part in enumerate((input_text[:, 0, :], input_img[:, 0, :], input_compress)):
-            pieces.append({"begin": begin_matrix, "end": end_matrix, "matrix": part,
+            pieces.append({"begin": begin_matrix, "end": end_matrix, "matrix": part, "order": "(j p) k -> p j k",
                            "operand": feat_mx, "k_pass": c})
         weights = []
         for weight, operand in ((Wr_img, wr_img_mx), (Wr_txt, wr_txt_mx), (Wl_img, wl_img_mx), (Wl_txt, wl_txt_mx)):
-            weights.append({"begin": begin_matrix, "end": end_matrix, "matrix": weight,
+            weights.append({"begin": begin_matrix, "end": end_matrix, "matrix": weight, "order": "(p j) k -> p j k",
                             "operand": operand, "k_pass": 0})
         pieces += weights
         pieces.insert(5, {"begin": load_biases, "end": turn_biases})
@@ -248,17 +249,22 @@ def tile_graphlearner_ib_pa_kernel(
                 in1=nodes[:, PAIRS:LOAD_NODES, :].rearrange("p n (q t) -> p n t q", t=PACK),
                 op=ADD,
             )
-            if ut < FOLDED_BLOCKS:
-                late.append([lambda: fold_pairs(block, load, pairs)])
-            else:
-                late.append([lambda: None, lambda: turn_sums(block, load, pairs, PAIRS)])
+            late.append([lambda: fold_pairs(block, load, pairs)])
 
         def fold_pairs(block, load, pairs):
             fours = four_sums.tile([P, PAIRS // 2, PACK, P], F32, name="fours")
             nc.vector.tensor_tensor(
                 out=fours, in0=pairs[:, 0 : PAIRS // 2], in1=pairs[:, PAIRS // 2 : PAIRS], op=ADD
             )
-            late.append([lambda: None] * TURN_LAG + [lambda: turn_sums(block, load, fours, PAIRS // 2)])
+            if block["ut"] < FOLDED_TWICE:
+                late.append([lambda: fold_fours(block, load, fours)])
+            else:
+                late.append([lambda: None] * TURN_LAG + [lambda: turn_sums(block, load, fours, PAIRS // 2)])
+
+        def fold_fours(block, load, fours):
+            eights = four_sums.tile([P, 1, PACK, P], F32, name="eights")
+            nc.vector.tensor_tensor(out=eights, in0=fours[:, 0:1], in1=fours[:, 1:2], op=ADD)
+            late.append([lambda: None] * (TURN_LAG - 1) + [lambda: turn_sums(block, load, eights, 1)])
 
         def turn_sums(block, load, sums, count):
             for t in range(PACK):
@@ -323,7 +329,7 @@ def tile_graphlearner_ib_pa_kernel(
 
         def permute(block):
             block["mean_rows"] = stage.tile([P, PACK, P], BF16, name="mean_rows", align_bytes=64)
-            nc.vector.tensor_copy(out=block["mean_rows"], in_=block["back"].rearrange("p (q t) -> p t q", t=PACK))
+            nc.scalar.copy(out=block["mean_rows"], in_=block["back"].rearrange("p (q t) -> p t q", t=PACK))
 
         def turn_forth(block):
             block["forth"] = prep_banks.tile([P, PACK, P], BF16, name="prep_bank")
@@ -334,13 +340,21 @@ def tile_graphlearner_ib_pa_kernel(
             block["mean_grouped"] = stage.tile([P, P, PACK], BF16, name="mean_grouped", align_bytes=64)
             nc.scalar.copy(out=block["mean_grouped"], in_=block["forth"].rearrange("p t b -> p b t"))
 
+        def turn_back_and_permute(block):
+            turn_back(block)
+            permute(block)
+
+        def turn_forth_and_group(block):
+            turn_forth(block)
+            group_means(block)
+
         def finish_steps(block):
             if block["split"] < P:
                 steps = [gather_last, quantise_mean]
             elif block["direct"]:
                 steps = [gather, quantise_mean]
             else:
-                steps = [round_means, turn_back, permute, turn_forth, group_means, quantise_mean]
+                steps = [round_means, turn_back_and_permute, turn_forth_and_group, quantise_mean]
             return [lambda step=step: step(block) for step in steps]
 
         def gather(block):
@@ -393,7 +407,8 @@ def tile_graphlearner_ib_pa_kernel(
                 )
                 result = results.tile([P, WIDTH // parts], F32, name="result")
                 nc.scalar.activation(out=result, in_=biased.rearrange("p r j -> p (r j)"), func=RELU)
-                nc.scalar.dma_start(out=out[ut * P : (ut + 1) * P, columns], in_=result)
+                queue = (nc.gpsimd, nc.gpsimd, nc.scalar, nc.sync)[ut]
+                queue.dma_start(out=out[ut * P : (ut + 1) * P, columns], in_=result)
 
         ctx.enter_context(tc.manual_schedule(engines={mybir.EngineType.PE}))
         user_queue, node_queue = [], []
@@ -420,6 +435,7 @@ def tile_graphlearner_ib_pa_kernel(
                 node_at += 1
         order += node_queue[node_at:]
 
+        fast = []
         waiting = []
         multiplied = set()
         begun = None
@@ -435,8 +451,10 @@ def tile_graphlearner_ib_pa_kernel(
                 if u_ready and ut not in multiplied and ("img", ut) in done and ("txt", ut) in done:
                     multiplied.add(ut)
                     tile = {"ut": ut}
-                    multiply(tile)
-                    waiting.append([lambda tile=tile: store(tile)])
+                    lag = 0 if ut == USER_TILES - 1 else TILE_LAG
+                    waiting.append(
+                        [lambda: None] * lag + [lambda tile=tile: multiply(tile), lambda tile=tile: store(tile)]
+                    )
 
         for block, load, first_load, last_load in order:
             piece = pieces.pop(0) if pieces else None
@@ -446,6 +464,7 @@ def tile_graphlearner_ib_pa_kernel(
                 block["sum_bank"] = sum_banks.tile([P, PACK, P], F32, name="sum_bank")
                 if block["split"] < P:
                     block["last_bank"] = sum_banks.tile([P, PACK, P], F32, name="sum_bank")
+            write_steps(fast)
             before = list(late)
             late.clear()
             block["add_load"](block, load)
@@ -457,13 +476,15 @@ def tile_graphlearner_ib_pa_kernel(
                 begun["end"](begun)
                 u_ready = u_ready or begun.get("ut") == USER_TILES - 1
             begun = piece
+            write_steps(fast)
             write_steps(waiting)
             write_tiles()
             if block["split"] < P and not last_load and load.stop == block["split"]:
                 waiting.append([lambda block=block: gather(block)])
             if last_load and block["kind"] == "txt":
-                waiting.append(finish_steps(block))
-        while late or waiting:
+                (waiting if block["direct"] else fast).append(finish_steps(block))
+        while late or fast or waiting:
+            write_steps(fast)
             before = list(late)
             late.clear()
             for steps in before:

@@ -11,6 +11,7 @@ FP8X4 = mybir.dt.float8_e4m3fn_x4
 ADD = mybir.AluOpType.add
 IS_GE = mybir.AluOpType.is_ge
 RELU = mybir.ActivationFunctionType.Relu
+IDENTITY = mybir.ActivationFunctionType.Identity
 
 P = 128
 PACK = 4
@@ -21,6 +22,7 @@ NODES = 24
 WIDTH = 512
 FEAT_PASSES = 3
 USER_TILES = USERS // P
+PRODUCTS = 4
 
 LOAD_NODES = 8
 PAIRS = LOAD_NODES // 2
@@ -30,10 +32,8 @@ ROW_TILES = 4
 LOAD_USERS = 32
 LAST_USERS = 32
 
-TURN_LAG = 2
-TILE_LAG = 1
-USER_LEAD = 3
-FOLDED_TWICE = 2
+TURN_LAGS = (2, 2, 2, 1)
+PASS_LAG = 2
 
 FLOPS = 2 * USERS * WIDTH * (FEAT_PASSES * K_PASS + 4 * K_PASS) + 2 * USERS * NODES * WIDTH
 
@@ -79,7 +79,7 @@ def tile_graphlearner_ib_pa_kernel(
         w_user_stage = ctx.enter_context(tc.tile_pool(name="w_user_stage", bufs=2 * FEAT_PASSES))
         four_sums = ctx.enter_context(tc.tile_pool(name="four_sums", bufs=5))
         pair_sums = ctx.enter_context(tc.tile_pool(name="pair_sums", bufs=3))
-        results = ctx.enter_context(tc.tile_pool(name="results", bufs=2))
+        results = ctx.enter_context(tc.tile_pool(name="results", bufs=3))
         prep_banks = ctx.enter_context(tc.psum_pool(name="prep_banks", bufs=3))
         sum_banks = ctx.enter_context(tc.psum_pool(name="sum_banks", bufs=4))
         out_banks = ctx.enter_context(tc.psum_pool(name="out_banks", bufs=1))
@@ -187,14 +187,14 @@ def tile_graphlearner_ib_pa_kernel(
 
         def end_u(piece):
             ut = piece["ut"]
-            nc.vector.tensor_tensor(
-                out=u_grouped[:, ut * P : (ut + 1) * P, :],
-                in0=piece["bank"].rearrange("p t b -> p b t"),
-                in1=b_user_columns.unsqueeze(1).to_broadcast([P, P, PACK]),
-                op=ADD,
-            )
+            for t in range(PACK):
+                nc.scalar.activation(
+                    out=u_grouped[:, ut * P : (ut + 1) * P, t], in_=piece["bank"][:, t, :],
+                    func=IDENTITY, bias=b_user_columns[:, t : t + 1],
+                )
             if ut == USER_TILES - 1:
                 quantise(nc, u_grouped, u_mx, 0, slice(0, USERS))
+                quantised["u"] = at["load"]
 
         def load_biases(piece):
             for row, vector in enumerate((b_user, bl_img, bl_txt)):
@@ -256,15 +256,7 @@ def tile_graphlearner_ib_pa_kernel(
             nc.vector.tensor_tensor(
                 out=fours, in0=pairs[:, 0 : PAIRS // 2], in1=pairs[:, PAIRS // 2 : PAIRS], op=ADD
             )
-            if block["ut"] < FOLDED_TWICE:
-                late.append([lambda: fold_fours(block, load, fours)])
-            else:
-                late.append([lambda: None] * TURN_LAG + [lambda: turn_sums(block, load, fours, PAIRS // 2)])
-
-        def fold_fours(block, load, fours):
-            eights = four_sums.tile([P, 1, PACK, P], F32, name="eights")
-            nc.vector.tensor_tensor(out=eights, in0=fours[:, 0:1], in1=fours[:, 1:2], op=ADD)
-            late.append([lambda: None] * (TURN_LAG - 1) + [lambda: turn_sums(block, load, eights, 1)])
+            late.append([lambda: None] * TURN_LAGS[block["ut"]] + [lambda: turn_sums(block, load, fours, PAIRS // 2)])
 
         def turn_sums(block, load, sums, count):
             for t in range(PACK):
@@ -316,7 +308,8 @@ def tile_graphlearner_ib_pa_kernel(
                             stop=(j == part_nodes - 1 and (last or not shared)),
                         )
 
-        done = []
+        quantised = {}
+        at = {"load": 0}
 
         def round_means(block):
             block["means"] = stage.tile([P, PACK, P], BF16, name="means", align_bytes=64)
@@ -375,23 +368,22 @@ def tile_graphlearner_ib_pa_kernel(
         def quantise_mean(block):
             users = slice(block["ut"] * P, (block["ut"] + 1) * P)
             quantise(nc, block["mean_grouped"], mean_mx[block["kind"]], 0, users)
-            done.append((block["kind"], block["ut"]))
+            quantised[block["kind"], block["ut"]] = at["load"]
 
         def multiply(tile):
             users = slice(tile["ut"] * P, (tile["ut"] + 1) * P)
-            acc = out_banks.tile([P, ROW_TILES, P], F32, name="acc")
-            products = (
+            i = tile["passes"]
+            left, right = (
                 (u_mx, wr_img_mx),
                 (u_mx, wr_txt_mx),
                 (mean_mx["img"], wl_img_mx),
                 (mean_mx["txt"], wl_txt_mx),
+            )[i]
+            mx_pass(
+                nc, tile["acc"].rearrange("p j r -> p (j r)"), left, 0, users, right, 0, slice(0, WIDTH),
+                start=(i == 0), stop=(i == PRODUCTS - 1),
             )
-            for i, (left, right) in enumerate(products):
-                mx_pass(
-                    nc, acc.rearrange("p j r -> p (j r)"), left, 0, users, right, 0, slice(0, WIDTH),
-                    start=(i == 0), stop=(i == len(products) - 1),
-                )
-            tile["acc"] = acc
+            tile["passes"] += 1
 
         def store(tile):
             ut = tile["ut"]
@@ -418,7 +410,7 @@ def tile_graphlearner_ib_pa_kernel(
         for ut in range(USER_TILES):
             last = ut == USER_TILES - 1
             block = {
-                "kind": "txt", "ut": ut, "part_nodes": 2 if ut < 2 else 3, "direct": last,
+                "kind": "txt", "ut": ut, "part_nodes": 2 if ut == 0 else 3, "direct": last,
                 "split": P - LAST_USERS if last else P, "add_load": add_nodes_load,
             }
             starts = list(range(0, P, LOAD_USERS))
@@ -427,36 +419,46 @@ def tile_graphlearner_ib_pa_kernel(
             for first, end in zip(starts, starts[1:] + [P]):
                 node_queue.append((block, range(first, end), first == 0, end == P))
         order = []
-        node_at = 0
         for i, entry in enumerate(user_queue):
             order.append(entry)
-            while node_at * len(user_queue) < (i - USER_LEAD) * len(node_queue):
-                order.append(node_queue[node_at])
-                node_at += 1
-        order += node_queue[node_at:]
+            order.append(node_queue[i])
+        order += node_queue[len(user_queue) :]
 
         fast = []
         waiting = []
-        multiplied = set()
         begun = None
-        u_ready = False
 
         def write_steps(lists):
             for steps in list(lists):
                 steps.pop(0)()
             lists[:] = [steps for steps in lists if steps]
 
-        def write_tiles():
-            for ut in range(USER_TILES):
-                if u_ready and ut not in multiplied and ("img", ut) in done and ("txt", ut) in done:
-                    multiplied.add(ut)
-                    tile = {"ut": ut}
-                    lag = 0 if ut == USER_TILES - 1 else TILE_LAG
-                    waiting.append(
-                        [lambda: None] * lag + [lambda tile=tile: multiply(tile), lambda tile=tile: store(tile)]
-                    )
+        banks = ((out_banks, "acc"), (prep_banks, "prep_bank"))
+        busy = set()
+        tiles = [{"ut": ut, "passes": 0} for ut in range(USER_TILES)]
+
+        def finish_tile(tile):
+            store(tile)
+            busy.remove(tile["ut"] % 2)
+
+        def write_products(lag):
+            for tile in tiles:
+                ut = tile["ut"]
+                for operand in ("u", "u", ("img", ut), ("txt", ut))[tile["passes"] :]:
+                    if operand not in quantised or at["load"] - quantised[operand] < lag:
+                        break
+                    if tile["passes"] == 0:
+                        if ut % 2 in busy:
+                            break
+                        busy.add(ut % 2)
+                        pool, name = banks[ut % 2]
+                        tile["acc"] = pool.tile([P, ROW_TILES, P], F32, name=name)
+                    multiply(tile)
+                    if tile["passes"] == PRODUCTS:
+                        waiting.append([lambda tile=tile: finish_tile(tile)])
 
         for block, load, first_load, last_load in order:
+            at["load"] += 1
             piece = pieces.pop(0) if pieces else None
             if piece is not None:
                 piece["begin"](piece)
@@ -465,6 +467,8 @@ def tile_graphlearner_ib_pa_kernel(
                 if block["split"] < P:
                     block["last_bank"] = sum_banks.tile([P, PACK, P], F32, name="sum_bank")
             write_steps(fast)
+            if block["split"] < P and last_load:
+                write_products(1)
             before = list(late)
             late.clear()
             block["add_load"](block, load)
@@ -474,11 +478,10 @@ def tile_graphlearner_ib_pa_kernel(
                     late.append(steps)
             if begun is not None:
                 begun["end"](begun)
-                u_ready = u_ready or begun.get("ut") == USER_TILES - 1
             begun = piece
             write_steps(fast)
             write_steps(waiting)
-            write_tiles()
+            write_products(PASS_LAG)
             if block["split"] < P and not last_load and load.stop == block["split"]:
                 waiting.append([lambda block=block: gather(block)])
             if last_load and block["kind"] == "txt":
@@ -492,4 +495,4 @@ def tile_graphlearner_ib_pa_kernel(
                 if steps:
                     late.append(steps)
             write_steps(waiting)
-            write_tiles()
+            write_products(0)

from contextlib import ExitStack

import concourse.mybir as mybir
from concourse.masks import make_identity

BF16 = mybir.dt.bfloat16
F32 = mybir.dt.float32
U32 = mybir.dt.uint32
U8 = mybir.dt.uint8
FP8X4 = mybir.dt.float8_e4m3fn_x4
ADD = mybir.AluOpType.add
IS_GE = mybir.AluOpType.is_ge
RELU = mybir.ActivationFunctionType.Relu
IDENTITY = mybir.ActivationFunctionType.Identity

P = 128
PACK = 4
K_PASS = P * PACK

USERS = 512
NODES = 24
WIDTH = 512
FEAT_PASSES = 3
USER_TILES = USERS // P
PRODUCTS = 4

LOAD_NODES = 8
PAIRS = LOAD_NODES // 2
USER_LOADS = NODES // LOAD_NODES
ROW_TILES = 4

LOAD_USERS = 32
LAST_USERS = 32

TURN_LAGS = (2, 2, 2, 1)
PASS_LAG = 2

FLOPS = 2 * USERS * WIDTH * (FEAT_PASSES * K_PASS + 4 * K_PASS) + 2 * USERS * NODES * WIDTH


def mx_tiles(pool, name, passes, columns):
    codes = pool.tile([P, passes, columns], U32, name=name + "_codes", align_bytes=64)
    scales = pool.tile([P, passes, columns], U8, name=name + "_scales", align_bytes=64)
    return codes, scales


def quantise(nc, grouped, operand, k_pass, columns):
    codes, scales = operand
    nc.vector.quantize_mx(
        out=codes[:, k_pass, columns].bitcast(FP8X4),
        scales=scales[:, k_pass, columns],
        in_=grouped.rearrange("p r t -> p (r t)"),
    )


def mx_pass(nc, acc, left, left_pass, left_columns, right, right_pass, right_columns, start, stop):
    nc.tensor.matmul_mx(
        out=acc,
        lhsT=left[0][:, left_pass, left_columns].bitcast(FP8X4),
        lhsT_scale=left[1][:, left_pass, left_columns],
        rhs=right[0][:, right_pass, right_columns].bitcast(FP8X4),
        rhs_scale=right[1][:, right_pass, right_columns],
        start=start,
        stop=stop,
    )


def tile_graphlearner_ib_pa_kernel(
    tc, input_text, input_img, input_compress, base_text_features, base_img_features,
    W_user, b_user, Wl_img, bl_img, Wr_img, Wl_txt, bl_txt, Wr_txt, out,
):
    nc = tc.nc
    with ExitStack() as ctx:
        const = ctx.enter_context(tc.tile_pool(name="const", bufs=1))
        keep = ctx.enter_context(tc.tile_pool(name="keep", bufs=1))
        user_rows = ctx.enter_context(tc.tile_pool(name="user_rows", bufs=6))
        loads = ctx.enter_context(tc.tile_pool(name="loads", bufs=9))
        stage = ctx.enter_context(tc.tile_pool(name="stage", bufs=3))
        w_user_stage = ctx.enter_context(tc.tile_pool(name="w_user_stage", bufs=2 * FEAT_PASSES))
        four_sums = ctx.enter_context(tc.tile_pool(name="four_sums", bufs=5))
        pair_sums = ctx.enter_context(tc.tile_pool(name="pair_sums", bufs=3))
        results = ctx.enter_context(tc.tile_pool(name="results", bufs=3))
        prep_banks = ctx.enter_context(tc.psum_pool(name="prep_banks", bufs=3))
        sum_banks = ctx.enter_context(tc.psum_pool(name="sum_banks", bufs=4))
        out_banks = ctx.enter_context(tc.psum_pool(name="out_banks", bufs=1))

        bias_rows = const.tile([P, WIDTH], BF16)
        nc.vector.memset(bias_rows, 0.0)
        identity = const.tile([P, P], BF16)
        make_identity(nc, identity)

        identity_f32 = const.tile([P, P], F32)
        make_identity(nc, identity_f32)
        zeros_f32 = const.tile([P, P], F32)
        nc.vector.memset(zeros_f32, 0.0)

        members = {}
        for part_nodes in (2, 3):
            user_parts = NODES // part_nodes
            members[part_nodes] = []
            for s in range(1 if part_nodes == 3 else LOAD_USERS * user_parts // P):
                first = s * P // user_parts
                count = (s * P + P - 1) // user_parts - first + 1
                offset = s * P - first * user_parts
                member_f32 = const.tile([P, count], F32, name=f"member_f32_{part_nodes}_{s}")
                nc.gpsimd.memset(member_f32, 1.0)
                nc.gpsimd.affine_select(
                    out=member_f32, in_=member_f32, pattern=[[-user_parts, count]],
                    compare_op=IS_GE, fill=0.0, base=offset, channel_multiplier=1,
                )
                nc.gpsimd.affine_select(
                    out=member_f32, in_=member_f32, pattern=[[user_parts, count]],
                    compare_op=IS_GE, fill=0.0, base=user_parts - 1 - offset, channel_multiplier=-1,
                )
                member = const.tile([P, count], BF16, name=f"member_{part_nodes}_{s}")
                nc.vector.tensor_copy(out=member, in_=member_f32)
                members[part_nodes].append((first, count, member))

        b_user_columns = const.tile([P, PACK], F32)
        bias_columns = const.tile([P, PACK], F32)
        out_bias = const.tile([P, PACK, P], F32)

        w_user_mx = mx_tiles(keep, "w_user", FEAT_PASSES, WIDTH)
        feat_mx = mx_tiles(keep, "feat", FEAT_PASSES, USERS)
        u_mx = mx_tiles(keep, "u", 1, USERS)
        wr_img_mx = mx_tiles(keep, "wr_img", 1, WIDTH)
        wr_txt_mx = mx_tiles(keep, "wr_txt", 1, WIDTH)
        wl_img_mx = mx_tiles(keep, "wl_img", 1, WIDTH)
        wl_txt_mx = mx_tiles(keep, "wl_txt", 1, WIDTH)
        mean_mx = {"img": mx_tiles(keep, "mean_img", 1, USERS), "txt": mx_tiles(keep, "mean_txt", 1, USERS)}
        u_grouped = keep.tile([P, USERS, PACK], BF16, align_bytes=64)

        def turn(words, first_word, grouped):
            bank = prep_banks.tile([P, 2, 2, P], F32, name="prep_bank")
            for j in range(2):
                for half in range(2):
                    nc.tensor.transpose(
                        bank[:, j, half, :],
                        words[:, j, first_word + half : first_word + K_PASS // 2 : 2],
                        identity_f32,
                    )
            nc.scalar.copy(
                out=grouped.bitcast(F32).rearrange("p (j r) h -> p j r h", j=2),
                in_=bank.rearrange("p j h r -> p j r h"),
            )

        def begin_w_user(piece):
            rows = loads.tile([P, 2, FEAT_PASSES * K_PASS], BF16, name="load")
            first = 2 * piece["half"]
            nc.sync.dma_start(out=rows, in_=W_user.rearrange("(p j) k -> p j k", j=PACK)[:, first : first + 2, :])
            piece["grouped"] = []
            for c in range(FEAT_PASSES):
                grouped = w_user_stage.tile([P, 2 * P, PACK], BF16, name="w_user_grouped", align_bytes=64)
                turn(rows[:].bitcast(F32), c * K_PASS // 2, grouped[:])
                piece["grouped"].append(grouped)

        def end_w_user(piece):
            columns = slice(piece["half"] * 2 * P, (piece["half"] + 1) * 2 * P)
            for c in range(FEAT_PASSES):
                quantise(nc, piece["grouped"][c], w_user_mx, c, columns)

        def begin_matrix(piece):
            rows = loads.tile([P, ROW_TILES, K_PASS], BF16, name="load")
            nc.sync.dma_start(out=rows, in_=piece["matrix"].rearrange(piece["order"], p=P))
            grouped = stage.tile([P, ROW_TILES * P, PACK], BF16, name="grouped", align_bytes=64)
            for pair in range(ROW_TILES // 2):
                turn(
                    rows[:, 2 * pair : 2 * pair + 2, :].bitcast(F32), 0,
                    grouped[:, 2 * pair * P : (2 * pair + 2) * P, :],
                )
            piece["grouped"] = grouped

        def end_matrix(piece):
            quantise(nc, piece["grouped"], piece["operand"], piece["k_pass"], slice(0, ROW_TILES * P))

        def begin_u(piece):
            ut = piece["ut"]
            u_bank = prep_banks.tile([P, PACK, P], F32, name="prep_bank")
            for t in range(PACK):
                for c in range(FEAT_PASSES):
                    mx_pass(
                        nc, u_bank[:, t, :], w_user_mx, c, slice(t * P, (t + 1) * P),
                        feat_mx, c, slice(ut * P, (ut + 1) * P),
                        start=(c == 0), stop=(c == FEAT_PASSES - 1),
                    )
            piece["bank"] = u_bank

        def end_u(piece):
            ut = piece["ut"]
            for t in range(PACK):
                nc.scalar.activation(
                    out=u_grouped[:, ut * P : (ut + 1) * P, t], in_=piece["bank"][:, t, :],
                    func=IDENTITY, bias=b_user_columns[:, t : t + 1],
                )
            if ut == USER_TILES - 1:
                quantise(nc, u_grouped, u_mx, 0, slice(0, USERS))
                quantised["u"] = at["load"]

        def load_biases(piece):
            for row, vector in enumerate((b_user, bl_img, bl_txt)):
                nc.sync.dma_start(out=bias_rows[row : row + 1, :], in_=vector.rearrange("(o n) -> o n", o=1))

        def turn_biases(piece):
            turned = prep_banks.tile([P, PACK, P], BF16, name="prep_bank")
            for t in range(PACK):
                nc.tensor.transpose(turned[:, t, :], bias_rows[:, t:WIDTH:PACK], identity)
            bias_parts = const.tile([P, 3, PACK], F32)
            nc.vector.tensor_copy(out=bias_parts, in_=turned[:, :, 0:3].rearrange("p t v -> p v t"))
            nc.vector.tensor_copy(out=b_user_columns, in_=bias_parts[:, 0, :])
            nc.vector.tensor_tensor(out=bias_columns, in0=bias_parts[:, 1, :], in1=bias_parts[:, 2, :], op=ADD)

        def begin_spread(piece):
            piece["bank"] = out_banks.tile([P, ROW_TILES, P], F32, name="acc")
            for j in range(PACK):
                nc.tensor.transpose(
                    piece["bank"][:, j, :], bias_columns[:, j : j + 1].to_broadcast([P, P]), identity_f32
                )

        def end_spread(piece):
            nc.vector.tensor_copy(out=out_bias, in_=piece["bank"])

        pieces = [{"begin": begin_w_user, "end": end_w_user, "half": half} for half in range(2)]
        for c, part in enumerate((input_text[:, 0, :], input_img[:, 0, :], input_compress)):
            pieces.append({"begin": begin_matrix, "end": end_matrix, "matrix": part, "order": "(j p) k -> p j k",
                           "operand": feat_mx, "k_pass": c})
        weights = []
        for weight, operand in ((Wr_img, wr_img_mx), (Wr_txt, wr_txt_mx), (Wl_img, wl_img_mx), (Wl_txt, wl_txt_mx)):
            weights.append({"begin": begin_matrix, "end": end_matrix, "matrix": weight, "order": "(p j) k -> p j k",
                            "operand": operand, "k_pass": 0})
        pieces += weights
        pieces.insert(5, {"begin": load_biases, "end": turn_biases})
        pieces.append({"begin": begin_spread, "end": end_spread})
        pieces += [{"begin": begin_u, "end": end_u, "ut": ut} for ut in range(USER_TILES)]

        late = []
        bases = {"img": base_img_features, "txt": base_text_features}

        def add_users_load(block, load):
            ut = block["ut"]
            nodes = user_rows.tile([P, LOAD_NODES, WIDTH], BF16, name="nodes")
            nc.sync.dma_start(
                out=nodes,
                in_=bases[block["kind"]][ut * P : (ut + 1) * P, load * LOAD_NODES : (load + 1) * LOAD_NODES, :],
            )
            pairs = pair_sums.tile([P, PAIRS, PACK, P], F32, name="pairs")
            nc.vector.tensor_tensor(
                out=pairs,
                in0=nodes[:, 0:PAIRS, :].rearrange("p n (q t) -> p n t q", t=PACK),
                in1=nodes[:, PAIRS:LOAD_NODES, :].rearrange("p n (q t) -> p n t q", t=PACK),
                op=ADD,
            )
            late.append([lambda: fold_pairs(block, load, pairs)])

        def fold_pairs(block, load, pairs):
            fours = four_sums.tile([P, PAIRS // 2, PACK, P], F32, name="fours")
            nc.vector.tensor_tensor(
                out=fours, in0=pairs[:, 0 : PAIRS // 2], in1=pairs[:, PAIRS // 2 : PAIRS], op=ADD
            )
            late.append([lambda: None] * TURN_LAGS[block["ut"]] + [lambda: turn_sums(block, load, fours, PAIRS // 2)])

        def turn_sums(block, load, sums, count):
            for t in range(PACK):
                for i in range(count):
                    nc.tensor.matmul(
                        out=block["sum_bank"][:, t, :],
                        lhsT=sums[:, i, t, :],
                        rhs=identity_f32,
                        is_transpose=True,
                        start=(load == 0 and t == 0 and i == 0),
                        stop=(load == USER_LOADS - 1 and t == PACK - 1 and i == count - 1),
                    )
            if load == USER_LOADS - 1:
                waiting.append(finish_steps(block))

        def add_nodes_load(block, users):
            part_nodes = block["part_nodes"]
            spans = len(users) * NODES // (P * part_nodes)
            first_node = (block["ut"] * P + users.start) * NODES
            rows = loads.tile([P, spans, part_nodes, WIDTH], BF16, name="load")
            nc.sync.dma_start(
                out=rows.rearrange("p s j h -> p s (j h)"),
                in_=bases[block["kind"]].rearrange("b n h -> (b n) h")[
                    first_node : first_node + len(users) * NODES, :
                ].rearrange("(s p j) h -> p s (j h)", p=P, j=part_nodes),
            )
            shared = part_nodes == 2
            if shared and users.start == 0:
                for t in range(PACK):
                    nc.tensor.matmul(
                        out=block["sum_bank"][:, t, :], lhsT=zeros_f32, rhs=identity_f32,
                        is_transpose=True, start=(t == 0), stop=False,
                    )
            for s in range(spans):
                first, count, member = members[part_nodes][s if shared else 0]
                first_user = users.start + (first if shared else s * count)
                bank = block["sum_bank"]
                if first_user >= block["split"]:
                    bank, first_user = block["last_bank"], first_user - block["split"]
                for t in range(PACK):
                    features = slice(t, WIDTH, PACK) if block["direct"] else slice(t * P, (t + 1) * P)
                    for j in range(part_nodes):
                        last = users.stop == P and s == spans - 1 and t == PACK - 1
                        nc.tensor.matmul(
                            out=bank[:, t, first_user : first_user + count],
                            lhsT=rows[:, s, j, features],
                            rhs=member,
                            start=(j == 0 and not shared),
                            stop=(j == part_nodes - 1 and (last or not shared)),
                        )

        quantised = {}
        at = {"load": 0}

        def round_means(block):
            block["means"] = stage.tile([P, PACK, P], BF16, name="means", align_bytes=64)
            nc.scalar.mul(out=block["means"], in_=block["sum_bank"], mul=1.0 / NODES)

        def turn_back(block):
            block["back"] = prep_banks.tile([P, WIDTH], BF16, name="prep_bank")
            for t in range(PACK):
                nc.tensor.transpose(block["back"][:, t * P : (t + 1) * P], block["means"][:, t, :], identity)

        def permute(block):
            block["mean_rows"] = stage.tile([P, PACK, P], BF16, name="mean_rows", align_bytes=64)
            nc.scalar.copy(out=block["mean_rows"], in_=block["back"].rearrange("p (q t) -> p t q", t=PACK))

        def turn_forth(block):
            block["forth"] = prep_banks.tile([P, PACK, P], BF16, name="prep_bank")
            for t in range(PACK):
                nc.tensor.transpose(block["forth"][:, t, :], block["mean_rows"][:, t, :], identity)

        def group_means(block):
            block["mean_grouped"] = stage.tile([P, P, PACK], BF16, name="mean_grouped", align_bytes=64)
            nc.scalar.copy(out=block["mean_grouped"], in_=block["forth"].rearrange("p t b -> p b t"))

        def turn_back_and_permute(block):
            turn_back(block)
            permute(block)

        def turn_forth_and_group(block):
            turn_forth(block)
            group_means(block)

        def finish_steps(block):
            if block["split"] < P:
                steps = [gather_last, quantise_mean]
            elif block["direct"]:
                steps = [gather, quantise_mean]
            else:
                steps = [round_means, turn_back_and_permute, turn_forth_and_group, quantise_mean]
            return [lambda step=step: step(block) for step in steps]

        def gather(block):
            block["mean_grouped"] = stage.tile([P, P, PACK], BF16, name="mean_grouped", align_bytes=64)
            nc.scalar.mul(
                out=block["mean_grouped"][:, 0 : block["split"], :],
                in_=block["sum_bank"][:, :, 0 : block["split"]].rearrange("p t b -> p b t"),
                mul=1.0 / NODES,
            )

        def gather_last(block):
            nc.scalar.mul(
                out=block["mean_grouped"][:, block["split"] : P, :],
                in_=block["last_bank"][:, :, 0 : P - block["split"]].rearrange("p t b -> p b t"),
                mul=1.0 / NODES,
            )

        def quantise_mean(block):
            users = slice(block["ut"] * P, (block["ut"] + 1) * P)
            quantise(nc, block["mean_grouped"], mean_mx[block["kind"]], 0, users)
            quantised[block["kind"], block["ut"]] = at["load"]

        def multiply(tile):
            users = slice(tile["ut"] * P, (tile["ut"] + 1) * P)
            i = tile["passes"]
            left, right = (
                (u_mx, wr_img_mx),
                (u_mx, wr_txt_mx),
                (mean_mx["img"], wl_img_mx),
                (mean_mx["txt"], wl_txt_mx),
            )[i]
            mx_pass(
                nc, tile["acc"].rearrange("p j r -> p (j r)"), left, 0, users, right, 0, slice(0, WIDTH),
                start=(i == 0), stop=(i == PRODUCTS - 1),
            )
            tile["passes"] += 1

        def store(tile):
            ut = tile["ut"]
            last = ut == USER_TILES - 1
            parts = 2 if last else 1
            for part in range(parts):
                rows = slice(part * P // parts, (part + 1) * P // parts)
                columns = slice(part * WIDTH // parts, (part + 1) * WIDTH // parts)
                biased = results.tile([P, P // parts, ROW_TILES], F32, name="biased")
                nc.vector.tensor_tensor(
                    out=biased, in0=tile["acc"][:, :, rows].rearrange("p j r -> p r j"),
                    in1=out_bias[:, :, rows].rearrange("p j r -> p r j"), op=ADD,
                )
                result = results.tile([P, WIDTH // parts], F32, name="result")
                nc.scalar.activation(out=result, in_=biased.rearrange("p r j -> p (r j)"), func=RELU)
                queue = (nc.gpsimd, nc.gpsimd, nc.scalar, nc.sync)[ut]
                queue.dma_start(out=out[ut * P : (ut + 1) * P, columns], in_=result)

        ctx.enter_context(tc.manual_schedule(engines={mybir.EngineType.PE}))
        user_queue, node_queue = [], []
        for ut in range(USER_TILES):
            block = {"kind": "img", "ut": ut, "split": P, "direct": True, "add_load": add_users_load}
            user_queue += [(block, load, load == 0, load == USER_LOADS - 1) for load in range(USER_LOADS)]
        for ut in range(USER_TILES):
            last = ut == USER_TILES - 1
            block = {
                "kind": "txt", "ut": ut, "part_nodes": 2 if ut == 0 else 3, "direct": last,
                "split": P - LAST_USERS if last else P, "add_load": add_nodes_load,
            }
            starts = list(range(0, P, LOAD_USERS))
            if last:
                starts.append(P - LOAD_USERS // 2)
            for first, end in zip(starts, starts[1:] + [P]):
                node_queue.append((block, range(first, end), first == 0, end == P))
        order = []
        for i, entry in enumerate(user_queue):
            order.append(entry)
            order.append(node_queue[i])
        order += node_queue[len(user_queue) :]

        fast = []
        waiting = []
        begun = None

        def write_steps(lists):
            for steps in list(lists):
                steps.pop(0)()
            lists[:] = [steps for steps in lists if steps]

        banks = ((out_banks, "acc"), (prep_banks, "prep_bank"))
        busy = set()
        tiles = [{"ut": ut, "passes": 0} for ut in range(USER_TILES)]

        def finish_tile(tile):
            store(tile)
            busy.remove(tile["ut"] % 2)

        def write_products(lag):
            for tile in tiles:
                ut = tile["ut"]
                for operand in ("u", "u", ("img", ut), ("txt", ut))[tile["passes"] :]:
                    if operand not in quantised or at["load"] - quantised[operand] < lag:
                        break
                    if tile["passes"] == 0:
                        if ut % 2 in busy:
                            break
                        busy.add(ut % 2)
                        pool, name = banks[ut % 2]
                        tile["acc"] = pool.tile([P, ROW_TILES, P], F32, name=name)
                    multiply(tile)
                    if tile["passes"] == PRODUCTS:
                        waiting.append([lambda tile=tile: finish_tile(tile)])

        for block, load, first_load, last_load in order:
            at["load"] += 1
            piece = pieces.pop(0) if pieces else None
            if piece is not None:
                piece["begin"](piece)
            if first_load:
                block["sum_bank"] = sum_banks.tile([P, PACK, P], F32, name="sum_bank")
                if block["split"] < P:
                    block["last_bank"] = sum_banks.tile([P, PACK, P], F32, name="sum_bank")
            write_steps(fast)
            if block["split"] < P and last_load:
                write_products(1)
            before = list(late)
            late.clear()
            block["add_load"](block, load)
            for steps in before:
                steps.pop(0)()
                if steps:
                    late.append(steps)
            if begun is not None:
                begun["end"](begun)
            begun = piece
            write_steps(fast)
            write_steps(waiting)
            write_products(PASS_LAG)
            if block["split"] < P and not last_load and load.stop == block["split"]:
                waiting.append([lambda block=block: gather(block)])
            if last_load and block["kind"] == "txt":
                (waiting if block["direct"] else fast).append(finish_steps(block))
        while late or fast or waiting:
            write_steps(fast)
            before = list(late)
            late.clear()
            for steps in before:
                steps.pop(0)()
                if steps:
                    late.append(steps)
            write_steps(waiting)
            write_products(0)
